import numpy as np
import ml_dtypes


def mxq(x, axis, fmt="e4m3"):
    dtype, down = {"e4m3": (ml_dtypes.float8_e4m3fn, 7), "e5m2": (ml_dtypes.float8_e5m2, 14)}[fmt]
    v = np.moveaxis(np.asarray(x, np.float32).astype(ml_dtypes.bfloat16).astype(np.float64), axis, -1)
    blocks = v.reshape(v.shape[:-1] + (-1, 32))
    amax = np.abs(blocks).max(-1, keepdims=True)
    byte = np.maximum(np.where(amax > 0, np.frexp(amax)[1] - 1 + 127, 0) - down, 1)
    scale = np.exp2(byte - 127.0)
    codes = (blocks / scale).astype(np.float32).astype(dtype).astype(np.float64)
    return np.moveaxis((codes * scale).reshape(v.shape), -1, axis)


WIDE = False


def mx_kscale(k):
    if not WIDE:
        return np.ones(k)
    levels = np.array([10, -10, 5, -5, 0])
    if k % 512:
        return np.exp2(np.random.permutation(np.resize(levels, k // 32))).repeat(32)
    a = np.empty((k // 512, 16))
    for p in range(k // 512):
        a[p, :8] = np.random.permutation(np.resize(levels, 8))
        for g in range(8):
            far = levels[np.abs(levels - a[p, g]) >= 10]
            a[p, g + 8] = far[np.random.randint(len(far))]
    return np.exp2(a.ravel()).repeat(32)


BF16 = ml_dtypes.bfloat16


def bf(x):
    return np.asarray(x, np.float32).astype(BF16)


def f64(x):
    return np.asarray(x).astype(np.float64)


B, I, H = 128, 2048, 2048
EPS = 1e-5


def sigmoid(v):
    return 1.0 / (1.0 + np.exp(-v))


def ln(v, g, b):
    m = v.mean(-1, keepdims=True)
    var = np.square(v - m).mean(-1, keepdims=True)
    return (v - m) / np.sqrt(var + EPS) * g + b


def draw0():
    s, t = mx_kscale(I), mx_kscale(H)
    d = {"x": bf(np.random.standard_normal((B, I)) * s), "h": bf(np.random.standard_normal((B, H)) * t)}
    for g in ("i", "c"):
        d["W" + g + "_w"] = bf(np.random.standard_normal((H, I)) / np.sqrt(I) / s[None, :])
        d["W" + g + "_b"] = bf(np.random.standard_normal(H) * 0.5)
        d["U" + g + "_w"] = bf(np.random.standard_normal((H, H)) / np.sqrt(H) / t[None, :])
        d["ln" + g + "_g"] = bf(1.0 + 0.2 * np.random.standard_normal(H))
        d["ln" + g + "_b"] = bf(0.2 * np.random.standard_normal(H))
    return d


def core(x, h, Wi_w, Wi_b, Ui_w, lni_g, lni_b, Wc_w, Wc_b, Uc_w, lnc_g, lnc_b):
    xq = mxq(f64(x), 1, "e4m3")
    hq = mxq(f64(h), 1, "e4m3")
    pre_i = (xq @ mxq(f64(Wi_w), 1, "e4m3").T) + f64(Wi_b) + (hq @ mxq(f64(Ui_w), 1, "e4m3").T)
    pre_c = (xq @ mxq(f64(Wc_w), 1, "e4m3").T) + f64(Wc_b) + (hq @ mxq(f64(Uc_w), 1, "e4m3").T)
    i = sigmoid(ln(pre_i, f64(lni_g), f64(lni_b)))
    c_tilde = np.tanh(ln(pre_c, f64(lnc_g), f64(lnc_b)))
    return i * c_tilde


def e4m3fn_bytes(y):
    return np.clip(np.asarray(y, np.float64), -448.0, 448.0).astype(np.float32).astype(ml_dtypes.float8_e4m3fn).view(np.uint8)


def e4m3fn_values(b):
    return np.asarray(b, np.uint8).view(ml_dtypes.float8_e4m3fn).astype(np.float64)


def setup_inputs():
    d = draw0()
    x0 = np.asarray(d['Wi_w']).astype(np.float64)
    s = (np.max(np.abs(x0), axis=(0,), keepdims=True) / 448.0).astype(np.float32)
    out = {}
    for k, v in d.items():
        if k == 'Wi_w':
            out['Wi_w_bytes'] = e4m3fn_bytes(x0 / s.astype(np.float64))
            out['Wi_w_scale'] = s
        else:
            out[k] = v
    return out


def reference(x, h, Wi_w_bytes, Wi_w_scale, Wi_b, Ui_w, lni_g, lni_b, Wc_w, Wc_b, Uc_w, lnc_g, lnc_b):
    return core(x, h, e4m3fn_values(Wi_w_bytes) * Wi_w_scale.astype(np.float64), Wi_b, Ui_w, lni_g, lni_b, Wc_w, Wc_b, Uc_w, lnc_g, lnc_b)

@@ -1,0 +1,531 @@
+from contextlib import ExitStack
+
+import concourse.masks as masks
+import concourse.mybir as mybir
+
+F32 = mybir.dt.float32
+BF16 = mybir.dt.bfloat16
+U32 = mybir.dt.uint32
+U8 = mybir.dt.uint8
+FP8 = mybir.dt.float8_e4m3fn
+FP8X4 = mybir.dt.float8_e4m3fn_x4
+ALU = mybir.AluOpType
+ACT = mybir.ActivationFunctionType
+AX = mybir.AxisListType
+
+P = 128
+K = 2048
+H = 2048
+NT = 512
+KS = 1024
+EPS = 1e-5
+FLOPS = 2 * 128 * 4096 * 4096
+
+AHEAD = 6
+BYTE_LEAD = 5.5
+SC2_KEY = -1.6
+RAW_BUFS = 6
+BYTE_BUFS = 4
+WIDE_BUFS = 3
+SORT_BUFS = 3
+GRP_BUFS = 2
+CODE_BUFS = 3
+TP_BUFS = 6
+SORT_CAP = 0
+SORT_FROM = 0
+VEC_KEYS = (15.1, 17.1)
+HEAD_ORDER = [
+    ("scale", 0), ("step", 0), ("act", "x"), ("rows", 0), ("scale", 1), ("step", 1), ("act", "h"), ("step", 2), ("scale", 2), ("scale", 3), ("step", 5),
+    ("step", 3), ("step", 4), ("step", 6), ("step", 10), ("step", 7), ("step", 8), ("step", 9),
+]
+PATTERN = "iccic" * 5 + "ic" + "iiiii"
+FIRST, LAST = "c", "i"
+WIDEN_CAP = 2
+
+
+def step_order():
+    i_seq = [(m, t, kh) for t in range(4) for kh in (0, 1) for m in ("Wi", "Ui")]
+    c_seq = [(m, t, kh) for t in range(4) for kh in (0, 1) for m in ("Wc", "Uc")]
+    order = []
+    for ch in PATTERN:
+        seq = i_seq if ch == "i" else c_seq
+        order.append(seq[0])
+        seq.remove(seq[0])
+    return order
+
+
+def tile_layernormlstmcell_pa_kernel(
+    tc, x, h, Wi_w_bytes, Wi_w_scale, Wi_b, Ui_w, lni_g, lni_b, Wc_w, Wc_b, Uc_w, lnc_g, lnc_b, out
+):
+    nc = tc.nc
+    steps = step_order()
+    n_steps = len(steps)
+    weights = {"Ui": Ui_w, "Wc": Wc_w, "Uc": Uc_w}
+    wi_steps = [i for i in range(n_steps) if steps[i][0] == "Wi"]
+
+    with ExitStack() as ctx:
+        const = ctx.enter_context(tc.tile_pool(name="const", bufs=1))
+        raw_pool = ctx.enter_context(tc.tile_pool(name="raw", bufs=RAW_BUFS))
+        byte_pool = ctx.enter_context(tc.tile_pool(name="bytes", bufs=BYTE_BUFS))
+        wide_pool = ctx.enter_context(tc.tile_pool(name="wide", bufs=WIDE_BUFS))
+        sort_pool = ctx.enter_context(tc.tile_pool(name="sorted", bufs=SORT_BUFS))
+        grp_pool = ctx.enter_context(tc.tile_pool(name="grp", bufs=GRP_BUFS))
+        code_pool = ctx.enter_context(tc.tile_pool(name="code", bufs=CODE_BUFS))
+        work = ctx.enter_context(tc.tile_pool(name="work", bufs=3))
+        psum = ctx.enter_context(tc.psum_pool(name="psum", bufs=1))
+        ctx.enter_context(tc.manual_schedule())
+
+        ident = const.tile([P, P], F32, name="ident")
+        masks.make_identity(nc, ident[:])
+        neg_half = const.tile([P, 1], F32, name="neg_half")
+        nc.gpsimd.memset(neg_half[:], -0.5)
+        warm = const.tile([P, 1], F32, name="warm")
+        nc.scalar.activation(out=warm[:], in_=neg_half[:], func=ACT.Sigmoid)
+
+        scale_bc = const.tile([P, K], F32, name="scale_bc")
+        vec_src = {"bias_i": Wi_b, "bias_c": Wc_b, "gain_i": lni_g, "gain_c": lnc_g, "shift_i": lni_b, "shift_c": lnc_b}
+        vec_names = ("bias_i", "bias_c", "gain_" + FIRST, "shift_" + FIRST, "gain_" + LAST, "shift_" + LAST)
+        ident_bf = const.tile([P, P], BF16, name="ident_bf")
+        masks.make_identity(nc, ident_bf[:])
+        vrows = const.tile([P, H], BF16, name="vrows")
+        nc.vector.memset(vrows[:], 0.0)
+        vec = {}
+        vec_sb = {}
+        for nm in vec_names[:4]:
+            vec_sb[nm] = const.tile([P, H], BF16, name=nm)
+        act_src = {"x": x, "h": h}
+        act_sb = {}
+        act_codes = {}
+        act_scales = {}
+        for nm in ("x", "h"):
+            act_sb[nm] = const.tile([P, K], BF16, name=nm + "_sb")
+            act_codes[nm] = const.tile([P, NT], U32, name=nm + "_codes", align_bytes=64)
+            act_scales[nm] = const.tile([P, NT], U8, name=nm + "_scales", align_bytes=64)
+        pre = {}
+        sums = {}
+        ssq = {}
+        small = {}
+        for g in ("i", "c"):
+            pre[g] = const.tile([P, H], F32, name="pre_" + g)
+            sums[g] = const.tile([P, 4], F32, name="sums_" + g)
+            ssq[g] = const.tile([P, 4], F32, name="ssq_" + g)
+            for nm in ("negc", "s012", "m012", "q012", "e0", "mean", "d", "e", "ve", "rstd"):
+                small[nm + g] = const.tile([P, 1], F32, name=nm + "_" + g)
+
+        src = {}
+        byt = {}
+        srt = {}
+        sorted_blocks = set()
+        grp = {}
+        codes = {}
+        scales = {}
+        acc = {}
+        passes = {}
+        turned = set()
+        raw_hist = []
+        byte_hist = []
+        widened = {"unit": 0}
+        vjobs = []
+        urgent = []
+        sjobs = []
+        flags = set()
+
+        def load_scale(c):
+            cols = slice(c * NT, (c + 1) * NT)
+            nc.sync.dma_start(out=scale_bc[:, cols], in_=Wi_w_scale[:, cols].rearrange("o k -> (o k)").partition_broadcast(P))
+
+        def load_act(nm):
+            nc.sync.dma_start(out=act_sb[nm][:], in_=act_src[nm])
+
+        def load_rows():
+            for j in (0, 1, 4, 5):
+                nc.sync.dma_start(out=vrows[j : j + 1, :], in_=vec_src[vec_names[j]].unsqueeze(0))
+
+        def load_vec(nm):
+            nc.sync.dma_start(out=vec_sb[nm][:], in_=vec_src[nm].partition_broadcast(P))
+            for half in (0, 1):
+                vec[(nm, half)] = vec_sb[nm][:, 2 * half * NT : 2 * (half + 1) * NT]
+
+        def spread(nm, half):
+            j = vec_names.index(nm)
+            ps = psum.tile([P, 2 * NT], BF16, name="tp", tag="tp", bufs=TP_BUFS)
+            for q in (0, 1):
+                c0 = (2 * half + q) * NT
+                nc.tensor.matmul(
+                    out=ps[:, q * NT : (q + 1) * NT], lhsT=ident_bf[:, j : j + 1].to_broadcast([P, P]), rhs=vrows[:, c0 : c0 + NT],
+                    start=True, stop=True,
+                )
+            if nm in vec_sb:
+                nc.scalar.copy(out=vec_sb[nm][:, 2 * half * NT : 2 * (half + 1) * NT], in_=ps[:])
+                vec[(nm, half)] = vec_sb[nm][:, 2 * half * NT : 2 * (half + 1) * NT]
+            else:
+                vec[(nm, half)] = ps
+
+        def vcols(nm, t):
+            return vec[(nm, t // 2)][:, (t % 2) * NT : (t % 2 + 1) * NT]
+
+        def can_fetch(i):
+            if steps[i][0] == "Wi":
+                n = len(byte_hist)
+                return n < BYTE_BUFS or widened["unit"] >= 8 * (n - BYTE_BUFS + 1)
+            n = len(raw_hist)
+            return n < RAW_BUFS or raw_hist[n - RAW_BUFS] in turned
+
+        def fetch(i):
+            m, t, kh = steps[i]
+            rows = slice(t * NT, (t + 1) * NT)
+            cols = slice(kh * KS, (kh + 1) * KS)
+            if m == "Wi":
+                wi_bytes = byte_pool.tile([P, 4, KS], U8, name="wi_bytes")
+                nc.sync.dma_start(out=wi_bytes[:], in_=Wi_w_bytes[rows, cols].rearrange("(r p) k -> p r k", p=P))
+                byt[i] = wi_bytes
+                byte_hist.append(i)
+            else:
+                raw = raw_pool.tile([P, 4, KS], BF16, name="raw")
+                nc.sync.dma_start(out=raw[:], in_=weights[m][rows, cols].rearrange("(r p) k -> p r k", p=P))
+                src[i] = raw
+                raw_hist.append(i)
+
+        keyed = [(-9.0, ("scale", 0)), (-8.0, ("step", 0)), (-7.0, ("act", "x")), (-6.0, ("scale", 1)), (1.5, ("act", "h"))]
+        keyed += [(SC2_KEY, ("scale", 2)), (SC2_KEY + 0.01, ("scale", 3)), (VEC_KEYS[0], ("vec", "gain_" + FIRST)), (VEC_KEYS[1], ("vec", "shift_" + FIRST))]
+        keyed += [(i - (BYTE_LEAD if steps[i][0] == "Wi" else 0.0), ("step", i)) for i in range(1, n_steps)]
+        plan = [e[1] for e in sorted(keyed)]
+        if HEAD_ORDER:
+            plan = list(HEAD_ORDER) + [e for e in plan if e not in HEAD_ORDER]
+        plan_at = {"i": 0}
+
+        def issue_loads(slot):
+            while plan_at["i"] < len(plan):
+                kind, what = plan[plan_at["i"]]
+                if kind == "step":
+                    if what > slot + AHEAD + (BYTE_LEAD if steps[what][0] == "Wi" else 0) or not can_fetch(what):
+                        return
+                    fetch(what)
+                elif kind == "scale":
+                    load_scale(what)
+                elif kind == "act":
+                    load_act(what)
+                elif kind == "rows":
+                    load_rows()
+                else:
+                    load_vec(what)
+                plan_at["i"] += 1
+
+        def widen_one():
+            u = widened["unit"]
+            if u >= 8 * len(wi_steps):
+                return False
+            j = u // 8
+            i = wi_steps[j]
+            if i not in byt:
+                return False
+            if u % 8 == 0:
+                if j >= WIDE_BUFS and wi_steps[j - WIDE_BUFS] not in turned:
+                    return False
+                wide = wide_pool.tile([P, 4, KS], BF16, name="wide")
+                src[i] = wide
+            gl = (u % 8) // 4
+            r = u % 4
+            kh = steps[i][2]
+            cols = slice(gl * NT, (gl + 1) * NT)
+            nc.vector.tensor_tensor(
+                out=src[i][:, r, cols],
+                in0=byt[i][:, r, cols].bitcast(FP8),
+                in1=scale_bc[:, kh * KS + gl * NT : kh * KS + (gl + 1) * NT],
+                op=ALU.mult,
+            )
+            widened["unit"] = u + 1
+            return True
+
+        def sort_one(first):
+            for i in (first, first + 1):
+                if i >= n_steps or i not in src or i in turned:
+                    continue
+                if steps[i][0] == "Wi" and widened["unit"] < 8 * (wi_steps.index(i) + 1):
+                    continue
+                for r in range(4):
+                    if (i, r) not in sorted_blocks:
+                        if i not in srt:
+                            s_t = sort_pool.tile([P, 4, 2, 2, P], F32, name="sorted")
+                            srt[i] = s_t
+                        nc.vector.tensor_copy(
+                            out=srt[i][:, r, :, :, :],
+                            in_=src[i][:].bitcast(F32)[:, r, :].rearrange("p (g j u) -> p g u j", g=2, u=2),
+                        )
+                        sorted_blocks.add((i, r))
+                        return True
+            return False
+
+        def turn_bank(word_aps, grp_words, b):
+            tp = psum.tile([P, 2, 2 * P], F32, name="tp", tag="tp", bufs=TP_BUFS)
+            for l in (0, 1):
+                for u in (0, 1):
+                    nc.tensor.transpose(out=tp[:, u, l * P : (l + 1) * P], in_=word_aps[l][u], identity=ident[:])
+            nc.scalar.copy(out=grp_words[:, 2 * P * b : 2 * P * (b + 1), :], in_=tp[:].rearrange("p u c -> p c u"))
+
+        def words_of(i, r, gl, u):
+            if (i, r) in sorted_blocks:
+                return srt[i][:, r, gl, u, :]
+            return src[i][:].bitcast(F32)[:, r, 256 * gl + u : 256 * (gl + 1) : 2]
+
+        def turn(i):
+            g_t = grp_pool.tile([P, 2, 4 * NT], BF16, name="grp", align_bytes=64)
+            grp[i] = g_t
+            for gl in (0, 1):
+                grp_words = g_t[:, gl, :].bitcast(F32).rearrange("p (c u) -> p c u", u=2)
+                for b in (0, 1):
+                    aps = [[words_of(i, 2 * b + l, gl, u) for u in (0, 1)] for l in (0, 1)]
+                    turn_bank(aps, grp_words, b)
+            turned.add(i)
+
+        def turn_act(nm):
+            words = act_sb[nm][:].bitcast(F32)
+            g_t = const.tile([P, 4 * NT], BF16, name="grp_" + nm, align_bytes=64)
+            grp[nm] = g_t
+            grp_words = g_t[:].bitcast(F32).rearrange("p (c u) -> p c u", u=2)
+            for b in (0, 1):
+                aps = [[words[:, 256 * (2 * b + l) + u : 256 * (2 * b + l + 1) : 2] for u in (0, 1)] for l in (0, 1)]
+                turn_bank(aps, grp_words, b)
+
+        def quantize_act(nm):
+            nc.vector.quantize_mx(out=act_codes[nm][:].bitcast(FP8X4), scales=act_scales[nm][:], in_=grp[nm][:])
+
+        def quantize(i):
+            c_t = code_pool.tile([P, 2 * NT], U32, name="codes", align_bytes=64)
+            s_t = code_pool.tile([P, 2 * NT], U8, name="scales", align_bytes=64)
+            codes[i] = c_t
+            scales[i] = s_t
+            if i + 1 < n_steps:
+                nc.vector.quantize_mx(out=c_t[:].bitcast(FP8X4), scales=s_t[:], in_=grp[i][:].rearrange("p g c -> p (g c)"))
+            else:
+                for gl in (0, 1):
+                    cols = slice(gl * NT, (gl + 1) * NT)
+                    nc.vector.quantize_mx(out=c_t[:, cols].bitcast(FP8X4), scales=s_t[:, cols], in_=grp[i][:, gl, :])
+
+        def multiply(i, gl, slot):
+            m, t, kh = steps[i]
+            g = m[1]
+            a = "x" if m[0] == "W" else "h"
+            done = passes.get((g, t), 0)
+            if done == 0:
+                assert t == 0 or ("empty", g, t - 1) in flags
+                acc_t = psum.tile([P, NT], F32, name="acc_" + g, tag="acc_" + g, bufs=1)
+                acc[g] = acc_t
+            kp = 2 * kh + gl
+            nc.tensor.matmul_mx(
+                out=acc[g][:],
+                lhsT=act_codes[a][:, kp * P : (kp + 1) * P].bitcast(FP8X4),
+                lhsT_scale=act_scales[a][:, kp * P : (kp + 1) * P],
+                rhs=codes[i][:, gl * NT : (gl + 1) * NT].bitcast(FP8X4),
+                rhs_scale=scales[i][:, gl * NT : (gl + 1) * NT],
+                start=(done == 0),
+                stop=(done == 7),
+            )
+            passes[(g, t)] = done + 1
+            if done == 7 and not (g == LAST and t == 3):
+                urgent.append([3 * (slot + 1), (), lambda: empty(g, t)])
+                sjobs.append([("empty", g, t), lambda: squares(g, t)])
+                if t == 2:
+                    vjobs.append([3 * (slot + 2), ("squares", g, 2), lambda: partial_sums(g)])
+                if t == 3:
+                    gate_jobs(g, slot + 1)
+
+        def empty(g, t):
+            cols = slice(t * NT, (t + 1) * NT)
+            nc.vector.scalar_tensor_tensor(
+                out=pre[g][:, cols], in0=acc[g][:], scalar=1.0, in1=vcols("bias_" + g, t),
+                op0=ALU.mult, op1=ALU.add, accum_out=sums[g][:, t : t + 1],
+            )
+            if t == 0:
+                nc.vector.tensor_scalar(out=small["negc" + g][:], in0=sums[g][:, 0:1], scalar1=-1.0 / NT, scalar2=None, op0=ALU.mult)
+            flags.add(("empty", g, t))
+
+        def squares(g, t):
+            cols = slice(t * NT, (t + 1) * NT)
+            junk = work.tile([P, NT], BF16, name="junk", bufs=2)
+            nc.scalar.activation(
+                out=junk[:], in_=pre[g][:, cols], func=ACT.Square, bias=small["negc" + g][:], scale=1.0,
+                accum_out=ssq[g][:, t : t + 1],
+            )
+            flags.add(("squares", g, t))
+
+        def partial_sums(g):
+            nc.vector.tensor_reduce(out=small["s012" + g][:], in_=sums[g][:, 0:3], axis=AX.X, op=ALU.add)
+            nc.vector.tensor_reduce(out=small["q012" + g][:], in_=ssq[g][:, 0:3], axis=AX.X, op=ALU.add)
+            nc.vector.tensor_scalar(out=small["m012" + g][:], in0=small["s012" + g][:], scalar1=1.0 / H, scalar2=None, op0=ALU.mult)
+            nc.vector.tensor_scalar(out=small["e0" + g][:], in0=small["q012" + g][:], scalar1=1.0 / H, scalar2=EPS, op0=ALU.mult, op1=ALU.add)
+            flags.add(("partial", g))
+
+        cen = {}
+        aff = {}
+        th = {}
+
+        def mean_of(g):
+            assert ("partial", g) in flags
+            nc.vector.scalar_tensor_tensor(
+                out=small["mean" + g][:], in0=sums[g][:, 3:4], scalar=1.0 / H, in1=small["m012" + g][:], op0=ALU.mult, op1=ALU.add
+            )
+
+        def shift_of(g):
+            nc.vector.tensor_tensor(out=small["d" + g][:], in0=small["mean" + g][:], in1=small["negc" + g][:], op=ALU.add)
+
+        def shift_sq(g):
+            nc.vector.scalar_tensor_tensor(
+                out=small["e" + g][:], in0=small["d" + g][:], scalar=small["d" + g][:], in1=small["e0" + g][:], op0=ALU.mult, op1=ALU.subtract
+            )
+
+        def rstd_of(g):
+            assert ("squares", g, 3) in flags
+            nc.vector.scalar_tensor_tensor(
+                out=small["ve" + g][:], in0=ssq[g][:, 3:4], scalar=1.0 / H, in1=small["e" + g][:], op0=ALU.mult, op1=ALU.subtract
+            )
+            nc.gpsimd.tensor_tensor(out=small["rstd" + g][:], in0=small["ve" + g][:], in1=neg_half[:], op=ALU.pow)
+
+        def centre(g, t):
+            cols = slice(t * NT, (t + 1) * NT)
+            c_t = work.tile([P, NT], F32, name="cen", bufs=4)
+            cen[(g, t)] = c_t
+            nc.vector.scalar_tensor_tensor(
+                out=c_t[:], in0=pre[g][:, cols], scalar=small["mean" + g][:], in1=vcols("gain_" + g, t), op0=ALU.subtract, op1=ALU.mult
+            )
+            flags.add(("centre", g, t))
+
+        def affine(g, t):
+            cols = slice(t * NT, (t + 1) * NT)
+            a_t = work.tile([P, NT], F32, name="aff", bufs=3)
+            aff[(g, t)] = a_t
+            nc.vector.scalar_tensor_tensor(
+                out=a_t[:], in0=cen[(g, t)][:], scalar=small["rstd" + g][:], in1=vcols("shift_" + g, t), op0=ALU.mult, op1=ALU.add
+            )
+            flags.add(("affine", g, t))
+
+        def squash(g, t):
+            func = ACT.Sigmoid if g == "i" else ACT.Tanh
+            if g == FIRST:
+                nc.scalar.activation(out=pre[g][:, t * NT : (t + 1) * NT], in_=aff[(g, t)][:], func=func)
+            else:
+                t_t = work.tile([P, NT], F32, name="th", bufs=3)
+                th[t] = t_t
+                nc.scalar.activation(out=t_t[:], in_=aff[(g, t)][:], func=func)
+
+        def product(t):
+            cols = slice(t * NT, (t + 1) * NT)
+            o_t = work.tile([P, NT], F32, name="o", bufs=4)
+            nc.vector.tensor_tensor(out=o_t[:], in0=pre[FIRST][:, cols], in1=th[t][:], op=ALU.mult)
+            nc.sync.dma_start(out=out[:, cols], in_=o_t[:])
+
+        def gate_jobs(g, slot):
+            def j1():
+                mean_of(g)
+                centre(g, 0)
+
+            def j2():
+                shift_of(g)
+                centre(g, 1)
+
+            def j3():
+                shift_sq(g)
+                centre(g, 2)
+
+            def j4():
+                assert ("centre", g, 2) in flags
+                rstd_of(g)
+                centre(g, 3)
+
+            vjobs.append([3 * slot + 1, ("empty", g, 3), j1])
+            vjobs.append([3 * slot + 2, ("centre", g, 0), j2])
+            vjobs.append([3 * slot + 3, ("centre", g, 1), j3])
+            vjobs.append([3 * slot + 4, ("squares", g, 3), j4])
+            for t in range(4):
+                vjobs.append([3 * slot + 5 + t, ("centre", g, 3), lambda t=t: affine(g, t)])
+                sjobs.append([("affine", g, t), lambda t=t: squash(g, t)])
+
+        widen_left = {"n": 0}
+
+        def vfill(pos):
+            able = [j for j in urgent + vjobs if j[0] <= pos and (not j[1] or j[1] in flags)]
+            if able:
+                if able[0] in urgent:
+                    urgent.remove(able[0])
+                else:
+                    vjobs.remove(able[0])
+                able[0][2]()
+            elif widen_left["n"] > 0 and widen_one():
+                widen_left["n"] -= 1
+
+        def sfill(n):
+            for k in range(n):
+                able = [j for j in sjobs if j[0] in flags]
+                if able:
+                    sjobs.remove(able[0])
+                    able[0][1]()
+
+        def ready(i):
+            if steps[i][0] == "Wi":
+                while widened["unit"] < 8 * (wi_steps.index(i) + 1):
+                    assert widen_one()
+
+        issue_loads(0)
+        for k in range(8):
+            widen_one()
+        turn_act("x")
+        quantize_act("x")
+        turn(0)
+        for nm in ("bias_i", "bias_c"):
+            spread(nm, 0)
+            spread(nm, 1)
+        ready(1)
+        turn(1)
+        turn_act("h")
+        quantize(0)
+        widen_one()
+        widen_one()
+        issue_loads(1)
+        for s in range(n_steps):
+            widen_left["n"] = WIDEN_CAP
+            if s + 2 < n_steps:
+                ready(s + 2)
+                turn(s + 2)
+            if s + 1 < n_steps:
+                quantize(s + 1)
+            if s == 0:
+                quantize_act("h")
+            vfill(3 * s)
+            vfill(3 * s + 1)
+            vfill(3 * s + 2)
+            sfill(1 if s + 2 < n_steps else 2)
+            if s + 1 == n_steps:
+                spread("gain_" + LAST, 0)
+            multiply(s, 0, s)
+            multiply(s, 1, s)
+            issue_loads(s + 2)
+        spread("gain_" + LAST, 1)
+        spread("shift_" + LAST, 0)
+        spread("shift_" + LAST, 1)
+
+        assert not vjobs and not urgent, len(vjobs)
+        g = LAST
+        empty(g, 3)
+        mean_of(g)
+        squares(g, 3)
+        sfill(16)
+        assert not sjobs
+        centre(g, 0)
+        shift_of(g)
+        centre(g, 1)
+        shift_sq(g)
+        rstd_of(g)
+        centre(g, 2)
+        centre(g, 3)
+        affine(g, 0)
+        affine(g, 1)
+        squash(g, 0)
+        affine(g, 2)
+        squash(g, 1)
+        product(0)
+        affine(g, 3)
+        squash(g, 2)
+        product(1)
+        squash(g, 3)
+        product(2)
+        product(3)

@@ -35,12 +35,17 @@ SORT_CAP = 0
 SORT_FROM = 0
 VEC_KEYS = (15.1, 17.1)
 HEAD_ORDER = [
-    ("scale", 0), ("step", 0), ("act", "x"), ("rows", 0), ("scale", 1), ("step", 1), ("act", "h"), ("step", 2), ("scale", 2), ("scale", 3), ("step", 5),
-    ("step", 3), ("step", 4), ("step", 6), ("step", 10), ("step", 7), ("step", 8), ("step", 9),
+    ("scale", 0), ("step", 0), ("act", "x"), ("scale", 1), ("step", 1), ("act", "h"), ("step", 2), ("scale", 2), ("scale", 3), ("step", 5),
+    ("step", 3), ("step", 4), ("vec", "bias_c"), ("step", 6), ("vec", "bias_i"), ("step", 10), ("step", 7), ("step", 8), ("step", 9), ("rows", 0),
 ]
 PATTERN = "iccic" * 5 + "ic" + "iiiii"
 FIRST, LAST = "c", "i"
 WIDEN_CAP = 2
+UW = 512
+PER = 4 * (KS // UW)
+BIAS_DMA = True
+GP_PRODUCTS = ()
+SWAP_BANK = False
 
 
 def step_order():
@@ -138,7 +143,7 @@ def tile_layernormlstmcell_pa_kernel(
             nc.sync.dma_start(out=act_sb[nm][:], in_=act_src[nm])
 
         def load_rows():
-            for j in (0, 1, 4, 5):
+            for j in (4, 5) if BIAS_DMA else (0, 1, 4, 5):
                 nc.sync.dma_start(out=vrows[j : j + 1, :], in_=vec_src[vec_names[j]].unsqueeze(0))
 
         def load_vec(nm):
@@ -167,7 +172,7 @@ def tile_layernormlstmcell_pa_kernel(
         def can_fetch(i):
             if steps[i][0] == "Wi":
                 n = len(byte_hist)
-                return n < BYTE_BUFS or widened["unit"] >= 8 * (n - BYTE_BUFS + 1)
+                return n < BYTE_BUFS or widened["unit"] >= PER * (n - BYTE_BUFS + 1)
             n = len(raw_hist)
             return n < RAW_BUFS or raw_hist[n - RAW_BUFS] in turned
 
@@ -213,25 +218,25 @@ def tile_layernormlstmcell_pa_kernel(
 
         def widen_one():
             u = widened["unit"]
-            if u >= 8 * len(wi_steps):
+            if u >= PER * len(wi_steps):
                 return False
-            j = u // 8
+            j = u // PER
             i = wi_steps[j]
             if i not in byt:
                 return False
-            if u % 8 == 0:
+            if u % PER == 0:
                 if j >= WIDE_BUFS and wi_steps[j - WIDE_BUFS] not in turned:
                     return False
                 wide = wide_pool.tile([P, 4, KS], BF16, name="wide")
                 src[i] = wide
-            gl = (u % 8) // 4
+            gl = (u % PER) // 4
             r = u % 4
             kh = steps[i][2]
-            cols = slice(gl * NT, (gl + 1) * NT)
+            cols = slice(gl * UW, (gl + 1) * UW)
             nc.vector.tensor_tensor(
                 out=src[i][:, r, cols],
                 in0=byt[i][:, r, cols].bitcast(FP8),
-                in1=scale_bc[:, kh * KS + gl * NT : kh * KS + (gl + 1) * NT],
+                in1=scale_bc[:, kh * KS + gl * UW : kh * KS + (gl + 1) * UW],
                 op=ALU.mult,
             )
             widened["unit"] = u + 1
@@ -241,7 +246,7 @@ def tile_layernormlstmcell_pa_kernel(
             for i in (first, first + 1):
                 if i >= n_steps or i not in src or i in turned:
                     continue
-                if steps[i][0] == "Wi" and widened["unit"] < 8 * (wi_steps.index(i) + 1):
+                if steps[i][0] == "Wi" and widened["unit"] < PER * (wi_steps.index(i) + 1):
                     continue
                 for r in range(4):
                     if (i, r) not in sorted_blocks:
@@ -271,11 +276,13 @@ def tile_layernormlstmcell_pa_kernel(
         def turn(i):
             g_t = grp_pool.tile([P, 2, 4 * NT], BF16, name="grp", align_bytes=64)
             grp[i] = g_t
-            for gl in (0, 1):
+            banks = [(gl, b) for gl in (0, 1) for b in (0, 1)]
+            if steps[i][0] == "Wi" and UW == KS:
+                banks = [(gl, b) for b in (0, 1) for gl in (0, 1)]
+            for gl, b in banks:
                 grp_words = g_t[:, gl, :].bitcast(F32).rearrange("p (c u) -> p c u", u=2)
-                for b in (0, 1):
-                    aps = [[words_of(i, 2 * b + l, gl, u) for u in (0, 1)] for l in (0, 1)]
-                    turn_bank(aps, grp_words, b)
+                aps = [[words_of(i, 2 * b + l, gl, u) for u in (0, 1)] for l in (0, 1)]
+                turn_bank(aps, grp_words, b)
             turned.add(i)
 
         def turn_act(nm):
@@ -309,11 +316,12 @@ def tile_layernormlstmcell_pa_kernel(
             done = passes.get((g, t), 0)
             if done == 0:
                 assert t == 0 or ("empty", g, t - 1) in flags
-                acc_t = psum.tile([P, NT], F32, name="acc_" + g, tag="acc_" + g, bufs=1)
-                acc[g] = acc_t
+                bank = FIRST if (SWAP_BANK and g == LAST and t == 3) else g
+                acc_t = psum.tile([P, NT], F32, name="acc_" + bank, tag="acc_" + bank, bufs=1)
+                acc[(g, t)] = acc_t
             kp = 2 * kh + gl
             nc.tensor.matmul_mx(
-                out=acc[g][:],
+                out=acc[(g, t)][:],
                 lhsT=act_codes[a][:, kp * P : (kp + 1) * P].bitcast(FP8X4),
                 lhsT_scale=act_scales[a][:, kp * P : (kp + 1) * P],
                 rhs=codes[i][:, gl * NT : (gl + 1) * NT].bitcast(FP8X4),
@@ -333,7 +341,7 @@ def tile_layernormlstmcell_pa_kernel(
         def empty(g, t):
             cols = slice(t * NT, (t + 1) * NT)
             nc.vector.scalar_tensor_tensor(
-                out=pre[g][:, cols], in0=acc[g][:], scalar=1.0, in1=vcols("bias_" + g, t),
+                out=pre[g][:, cols], in0=acc[(g, t)][:], scalar=1.0, in1=vcols("bias_" + g, t),
                 op0=ALU.mult, op1=ALU.add, accum_out=sums[g][:, t : t + 1],
             )
             if t == 0:
@@ -411,7 +419,8 @@ def tile_layernormlstmcell_pa_kernel(
         def product(t):
             cols = slice(t * NT, (t + 1) * NT)
             o_t = work.tile([P, NT], F32, name="o", bufs=4)
-            nc.vector.tensor_tensor(out=o_t[:], in0=pre[FIRST][:, cols], in1=th[t][:], op=ALU.mult)
+            eng = nc.gpsimd if t in GP_PRODUCTS else nc.vector
+            eng.tensor_tensor(out=o_t[:], in0=pre[FIRST][:, cols], in1=th[t][:], op=ALU.mult)
             nc.sync.dma_start(out=out[:, cols], in_=o_t[:])
 
         def gate_jobs(g, slot):
@@ -462,24 +471,24 @@ def tile_layernormlstmcell_pa_kernel(
 
         def ready(i):
             if steps[i][0] == "Wi":
-                while widened["unit"] < 8 * (wi_steps.index(i) + 1):
+                while widened["unit"] < PER * (wi_steps.index(i) + 1):
                     assert widen_one()
 
         issue_loads(0)
-        for k in range(8):
+        for k in range(PER):
             widen_one()
         turn_act("x")
         quantize_act("x")
         turn(0)
-        for nm in ("bias_i", "bias_c"):
+        for nm in () if BIAS_DMA else ("bias_i", "bias_c"):
             spread(nm, 0)
             spread(nm, 1)
         ready(1)
         turn(1)
         turn_act("h")
         quantize(0)
-        widen_one()
-        widen_one()
+        for k in range(PER // 4):
+            widen_one()
         issue_loads(1)
         for s in range(n_steps):
             widen_left["n"] = WIDEN_CAP

@@ -273,16 +273,19 @@ def tile_layernormlstmcell_pa_kernel(
                 return srt[i][:, r, gl, u, :]
             return src[i][:].bitcast(F32)[:, r, 256 * gl + u : 256 * (gl + 1) : 2]
 
-        def turn(i):
+        def turn(i, halfway=None):
             g_t = grp_pool.tile([P, 2, 4 * NT], BF16, name="grp", align_bytes=64)
             grp[i] = g_t
             banks = [(gl, b) for gl in (0, 1) for b in (0, 1)]
             if steps[i][0] == "Wi" and UW == KS:
                 banks = [(gl, b) for b in (0, 1) for gl in (0, 1)]
-            for gl, b in banks:
+            for n_bank in range(4):
+                gl, b = banks[n_bank]
                 grp_words = g_t[:, gl, :].bitcast(F32).rearrange("p (c u) -> p c u", u=2)
                 aps = [[words_of(i, 2 * b + l, gl, u) for u in (0, 1)] for l in (0, 1)]
                 turn_bank(aps, grp_words, b)
+                if n_bank == 1 and halfway:
+                    halfway()
             turned.add(i)
 
         def turn_act(nm):
@@ -492,9 +495,11 @@ def tile_layernormlstmcell_pa_kernel(
         issue_loads(1)
         for s in range(n_steps):
             widen_left["n"] = WIDEN_CAP
+            while [j for j in urgent if j[0] <= 3 * s]:
+                vfill(3 * s)
             if s + 2 < n_steps:
                 ready(s + 2)
-                turn(s + 2)
+                turn(s + 2, lambda: multiply(s, 0, s))
             if s + 1 < n_steps:
                 quantize(s + 1)
             if s == 0:
@@ -505,13 +510,16 @@ def tile_layernormlstmcell_pa_kernel(
             sfill(1 if s + 2 < n_steps else 2)
             if s + 1 == n_steps:
                 spread("gain_" + LAST, 0)
-            multiply(s, 0, s)
+            if s + 2 >= n_steps:
+                multiply(s, 0, s)
             multiply(s, 1, s)
             issue_loads(s + 2)
         spread("gain_" + LAST, 1)
         spread("shift_" + LAST, 0)
         spread("shift_" + LAST, 1)
 
+        for k in range(len(vjobs)):
+            vfill(3 * n_steps)
         assert not vjobs and not urgent, len(vjobs)
         g = LAST
         empty(g, 3)

@@ -41,11 +41,12 @@ HEAD_ORDER = [
 PATTERN = "iccic" * 5 + "ic" + "iiiii"
 FIRST, LAST = "c", "i"
 WIDEN_CAP = 2
+FINE_STEPS = 1
 UW = 512
 PER = 4 * (KS // UW)
 BIAS_DMA = True
-GP_PRODUCTS = ()
-SWAP_BANK = False
+GP_PRODUCTS = (0, 1)
+SWAP_BANK = True
 
 
 def step_order():
@@ -67,6 +68,12 @@ def tile_layernormlstmcell_pa_kernel(
     n_steps = len(steps)
     weights = {"Ui": Ui_w, "Wc": Wc_w, "Uc": Uc_w}
     wi_steps = [i for i in range(n_steps) if steps[i][0] == "Wi"]
+    units = []
+    units_upto = {}
+    for j in range(len(wi_steps)):
+        width = NT if j < FINE_STEPS else KS
+        units += [(wi_steps[j], r, c0, width) for c0 in range(0, KS, width) for r in range(4)]
+        units_upto[wi_steps[j]] = len(units)
 
     with ExitStack() as ctx:
         const = ctx.enter_context(tc.tile_pool(name="const", bufs=1))
@@ -80,6 +87,8 @@ def tile_layernormlstmcell_pa_kernel(
         psum = ctx.enter_context(tc.psum_pool(name="psum", bufs=1))
         ctx.enter_context(tc.manual_schedule())
 
+        scale_rows = const.tile([P, P], F32, name="scale_rows")
+        nc.gpsimd.memset(scale_rows[:], 0.0)
         ident = const.tile([P, P], F32, name="ident")
         masks.make_identity(nc, ident[:])
         neg_half = const.tile([P, 1], F32, name="neg_half")
@@ -88,6 +97,7 @@ def tile_layernormlstmcell_pa_kernel(
         nc.scalar.activation(out=warm[:], in_=neg_half[:], func=ACT.Sigmoid)
 
         scale_bc = const.tile([P, K], F32, name="scale_bc")
+        scale_cols = const.tile([P, 16], F32, name="scale_cols")
         vec_src = {"bias_i": Wi_b, "bias_c": Wc_b, "gain_i": lni_g, "gain_c": lnc_g, "shift_i": lni_b, "shift_c": lnc_b}
         vec_names = ("bias_i", "bias_c", "gain_" + FIRST, "shift_" + FIRST, "gain_" + LAST, "shift_" + LAST)
         ident_bf = const.tile([P, P], BF16, name="ident_bf")
@@ -136,8 +146,20 @@ def tile_layernormlstmcell_pa_kernel(
         flags = set()
 
         def load_scale(c):
-            cols = slice(c * NT, (c + 1) * NT)
-            nc.sync.dma_start(out=scale_bc[:, cols], in_=Wi_w_scale[:, cols].rearrange("o k -> (o k)").partition_broadcast(P))
+            if c == 0:
+                nc.sync.dma_start(out=scale_rows[0:16, :], in_=Wi_w_scale.rearrange("o (c j) -> (o c) j", j=P))
+
+        def turn_scales():
+            tp = psum.tile([P, 2, 2 * P], F32, name="tp", tag="tp", bufs=TP_BUFS)
+            nc.tensor.transpose(out=tp[:, 0, 0:P], in_=scale_rows[:], identity=ident[:])
+            nc.scalar.copy(out=scale_cols[:], in_=tp[:, 0, 0:16])
+
+        def spread_scales(q):
+            tp = psum.tile([P, 2, 2 * P], F32, name="tp", tag="tp", bufs=TP_BUFS)
+            for l in range(4):
+                c = 4 * q + l
+                nc.tensor.transpose(out=tp[:, l // 2, (l % 2) * P : (l % 2 + 1) * P], in_=scale_cols[:, c : c + 1].to_broadcast([P, P]), identity=ident[:])
+            nc.scalar.copy(out=scale_bc[:, q * NT : (q + 1) * NT], in_=tp[:].rearrange("p a b -> p (a b)"))
 
         def load_act(nm):
             nc.sync.dma_start(out=act_sb[nm][:], in_=act_src[nm])
@@ -172,7 +194,7 @@ def tile_layernormlstmcell_pa_kernel(
         def can_fetch(i):
             if steps[i][0] == "Wi":
                 n = len(byte_hist)
-                return n < BYTE_BUFS or widened["unit"] >= PER * (n - BYTE_BUFS + 1)
+                return n < BYTE_BUFS or widened["unit"] >= units_upto[byte_hist[n - BYTE_BUFS]]
             n = len(raw_hist)
             return n < RAW_BUFS or raw_hist[n - RAW_BUFS] in turned
 
@@ -218,35 +240,32 @@ def tile_layernormlstmcell_pa_kernel(
 
         def widen_one():
             u = widened["unit"]
-            if u >= PER * len(wi_steps):
-                return False
-            j = u // PER
-            i = wi_steps[j]
+            if u >= len(units):
+                return 0
+            i, r, c0, width = units[u]
+            j = wi_steps.index(i)
             if i not in byt:
-                return False
-            if u % PER == 0:
+                return 0
+            if i not in src:
                 if j >= WIDE_BUFS and wi_steps[j - WIDE_BUFS] not in turned:
-                    return False
+                    return 0
                 wide = wide_pool.tile([P, 4, KS], BF16, name="wide")
                 src[i] = wide
-            gl = (u % PER) // 4
-            r = u % 4
             kh = steps[i][2]
-            cols = slice(gl * UW, (gl + 1) * UW)
             nc.vector.tensor_tensor(
-                out=src[i][:, r, cols],
-                in0=byt[i][:, r, cols].bitcast(FP8),
-                in1=scale_bc[:, kh * KS + gl * UW : kh * KS + (gl + 1) * UW],
+                out=src[i][:, r, c0 : c0 + width],
+                in0=byt[i][:, r, c0 : c0 + width].bitcast(FP8),
+                in1=scale_bc[:, kh * KS + c0 : kh * KS + c0 + width],
                 op=ALU.mult,
             )
             widened["unit"] = u + 1
-            return True
+            return width // NT
 
         def sort_one(first):
             for i in (first, first + 1):
                 if i >= n_steps or i not in src or i in turned:
                     continue
-                if steps[i][0] == "Wi" and widened["unit"] < PER * (wi_steps.index(i) + 1):
+                if steps[i][0] == "Wi" and widened["unit"] < units_upto[i]:
                     continue
                 for r in range(4):
                     if (i, r) not in sorted_blocks:
@@ -277,7 +296,7 @@ def tile_layernormlstmcell_pa_kernel(
             g_t = grp_pool.tile([P, 2, 4 * NT], BF16, name="grp", align_bytes=64)
             grp[i] = g_t
             banks = [(gl, b) for gl in (0, 1) for b in (0, 1)]
-            if steps[i][0] == "Wi" and UW == KS:
+            if steps[i][0] == "Wi" and wi_steps.index(i) >= FINE_STEPS:
                 banks = [(gl, b) for b in (0, 1) for gl in (0, 1)]
             for n_bank in range(4):
                 gl, b = banks[n_bank]
@@ -335,10 +354,13 @@ def tile_layernormlstmcell_pa_kernel(
             passes[(g, t)] = done + 1
             if done == 7 and not (g == LAST and t == 3):
                 urgent.append([3 * (slot + 1), (), lambda: empty(g, t)])
+                if t == 3:
+                    sjobs.append([("empty", g, 3), lambda: mean_on_scalar(g)])
                 sjobs.append([("empty", g, t), lambda: squares(g, t)])
                 if t == 2:
-                    vjobs.append([3 * (slot + 2), ("squares", g, 2), lambda: partial_sums(g)])
+                    sjobs.append([("squares", g, 2), lambda: partial_sums(g)])
                 if t == 3:
+                    sjobs.append([("squares", g, 3), lambda: rstd_on_scalar(g)])
                     gate_jobs(g, slot + 1)
 
         def empty(g, t):
@@ -347,13 +369,13 @@ def tile_layernormlstmcell_pa_kernel(
                 out=pre[g][:, cols], in0=acc[(g, t)][:], scalar=1.0, in1=vcols("bias_" + g, t),
                 op0=ALU.mult, op1=ALU.add, accum_out=sums[g][:, t : t + 1],
             )
-            if t == 0:
-                nc.vector.tensor_scalar(out=small["negc" + g][:], in0=sums[g][:, 0:1], scalar1=-1.0 / NT, scalar2=None, op0=ALU.mult)
             flags.add(("empty", g, t))
 
         def squares(g, t):
             cols = slice(t * NT, (t + 1) * NT)
             junk = work.tile([P, NT], BF16, name="junk", bufs=2)
+            if t == 0:
+                nc.scalar.activation(out=small["negc" + g][:], in_=sums[g][:, 0:1], func=ACT.Copy, scale=-1.0 / NT)
             nc.scalar.activation(
                 out=junk[:], in_=pre[g][:, cols], func=ACT.Square, bias=small["negc" + g][:], scale=1.0,
                 accum_out=ssq[g][:, t : t + 1],
@@ -361,11 +383,25 @@ def tile_layernormlstmcell_pa_kernel(
             flags.add(("squares", g, t))
 
         def partial_sums(g):
-            nc.vector.tensor_reduce(out=small["s012" + g][:], in_=sums[g][:, 0:3], axis=AX.X, op=ALU.add)
-            nc.vector.tensor_reduce(out=small["q012" + g][:], in_=ssq[g][:, 0:3], axis=AX.X, op=ALU.add)
-            nc.vector.tensor_scalar(out=small["m012" + g][:], in0=small["s012" + g][:], scalar1=1.0 / H, scalar2=None, op0=ALU.mult)
-            nc.vector.tensor_scalar(out=small["e0" + g][:], in0=small["q012" + g][:], scalar1=1.0 / H, scalar2=EPS, op0=ALU.mult, op1=ALU.add)
+            j_s = work.tile([P, 4], F32, name="junk_s", bufs=2)
+            nc.scalar.activation(out=j_s[:, 0:3], in_=sums[g][:, 0:3], func=ACT.Copy, scale=1.0 / H, accum_out=small["m012" + g][:])
+            j_q = work.tile([P, 4], F32, name="junk_q", bufs=2)
+            nc.scalar.activation(out=j_q[:, 0:3], in_=ssq[g][:, 0:3], func=ACT.Copy, scale=1.0 / H, bias=EPS / 3.0, accum_out=small["e0" + g][:])
             flags.add(("partial", g))
+
+        def mean_on_scalar(g):
+            assert ("partial", g) in flags
+            nc.scalar.activation(out=small["mean" + g][:], in_=sums[g][:, 3:4], func=ACT.Identity, scale=1.0 / H, bias=small["m012" + g][:])
+            flags.add(("mean", g))
+
+        def rstd_on_scalar(g):
+            assert ("squares", g, 3) in flags
+            nc.scalar.activation(out=small["d" + g][:], in_=small["mean" + g][:], func=ACT.Identity, scale=1.0, bias=small["negc" + g][:])
+            nc.scalar.activation(out=small["s012" + g][:], in_=small["d" + g][:], func=ACT.Square)
+            nc.scalar.activation(out=small["e" + g][:], in_=ssq[g][:, 3:4], func=ACT.Identity, scale=1.0 / H, bias=small["e0" + g][:])
+            nc.scalar.activation(out=small["ve" + g][:], in_=small["s012" + g][:], func=ACT.Identity, scale=-1.0, bias=small["e" + g][:])
+            nc.gpsimd.tensor_tensor(out=small["rstd" + g][:], in0=small["ve" + g][:], in1=neg_half[:], op=ALU.pow)
+            flags.add(("rstd", g))
 
         cen = {}
         aff = {}
@@ -415,7 +451,7 @@ def tile_layernormlstmcell_pa_kernel(
             if g == FIRST:
                 nc.scalar.activation(out=pre[g][:, t * NT : (t + 1) * NT], in_=aff[(g, t)][:], func=func)
             else:
-                t_t = work.tile([P, NT], F32, name="th", bufs=3)
+                t_t = work.tile([P, NT], F32, name="th", bufs=4)
                 th[t] = t_t
                 nc.scalar.activation(out=t_t[:], in_=aff[(g, t)][:], func=func)
 
@@ -427,29 +463,10 @@ def tile_layernormlstmcell_pa_kernel(
             nc.sync.dma_start(out=out[:, cols], in_=o_t[:])
 
         def gate_jobs(g, slot):
-            def j1():
-                mean_of(g)
-                centre(g, 0)
-
-            def j2():
-                shift_of(g)
-                centre(g, 1)
-
-            def j3():
-                shift_sq(g)
-                centre(g, 2)
-
-            def j4():
-                assert ("centre", g, 2) in flags
-                rstd_of(g)
-                centre(g, 3)
-
-            vjobs.append([3 * slot + 1, ("empty", g, 3), j1])
-            vjobs.append([3 * slot + 2, ("centre", g, 0), j2])
-            vjobs.append([3 * slot + 3, ("centre", g, 1), j3])
-            vjobs.append([3 * slot + 4, ("squares", g, 3), j4])
             for t in range(4):
-                vjobs.append([3 * slot + 5 + t, ("centre", g, 3), lambda t=t: affine(g, t)])
+                vjobs.append([3 * slot + 1 + t, ("mean", g), lambda t=t: centre(g, t)])
+            for t in range(4):
+                vjobs.append([3 * slot + 5 + t, ("rstd", g), lambda t=t: affine(g, t)])
                 sjobs.append([("affine", g, t), lambda t=t: squash(g, t)])
 
         widen_left = {"n": 0}
@@ -462,8 +479,8 @@ def tile_layernormlstmcell_pa_kernel(
                 else:
                     vjobs.remove(able[0])
                 able[0][2]()
-            elif widen_left["n"] > 0 and widen_one():
-                widen_left["n"] -= 1
+            elif widen_left["n"] > 0:
+                widen_left["n"] -= widen_one()
 
         def sfill(n):
             for k in range(n):
@@ -474,11 +491,14 @@ def tile_layernormlstmcell_pa_kernel(
 
         def ready(i):
             if steps[i][0] == "Wi":
-                while widened["unit"] < PER * (wi_steps.index(i) + 1):
+                while widened["unit"] < units_upto[i]:
                     assert widen_one()
 
         issue_loads(0)
-        for k in range(PER):
+        turn_scales()
+        for q in range(4):
+            spread_scales(q)
+        for k in range(8):
             widen_one()
         turn_act("x")
         quantize_act("x")
@@ -490,8 +510,7 @@ def tile_layernormlstmcell_pa_kernel(
         turn(1)
         turn_act("h")
         quantize(0)
-        for k in range(PER // 4):
-            widen_one()
+        widen_one()
         issue_loads(1)
         for s in range(n_steps):
             widen_left["n"] = WIDEN_CAP
@@ -504,10 +523,9 @@ def tile_layernormlstmcell_pa_kernel(
                 quantize(s + 1)
             if s == 0:
                 quantize_act("h")
-            vfill(3 * s)
-            vfill(3 * s + 1)
-            vfill(3 * s + 2)
-            sfill(1 if s + 2 < n_steps else 2)
+            for k in range(3):
+                vfill(3 * s + k)
+                sfill(1)
             if s + 1 == n_steps:
                 spread("gain_" + LAST, 0)
             if s + 2 >= n_steps:
@@ -533,16 +551,16 @@ def tile_layernormlstmcell_pa_kernel(
         shift_sq(g)
         rstd_of(g)
         centre(g, 2)
-        centre(g, 3)
         affine(g, 0)
-        affine(g, 1)
         squash(g, 0)
-        affine(g, 2)
+        affine(g, 1)
         squash(g, 1)
         product(0)
-        affine(g, 3)
+        centre(g, 3)
+        affine(g, 2)
         squash(g, 2)
         product(1)
+        affine(g, 3)
         squash(g, 3)
         product(2)
         product(3)

@@ -33,10 +33,11 @@ CODE_BUFS = 3
 TP_BUFS = 6
 SORT_CAP = 0
 SORT_FROM = 0
-VEC_KEYS = (15.1, 17.1)
+VEC_KEYS = (23.1, 25.1)
+BIAS_LEAD = 2.5
 HEAD_ORDER = [
     ("scale", 0), ("step", 0), ("act", "x"), ("scale", 1), ("step", 1), ("act", "h"), ("step", 2), ("scale", 2), ("scale", 3), ("step", 5),
-    ("step", 3), ("step", 4), ("vec", "bias_c"), ("step", 6), ("vec", "bias_i"), ("step", 10), ("step", 7), ("step", 8), ("step", 9), ("rows", 0),
+    ("step", 3), ("step", 4), ("step", 6), ("step", 10), ("step", 7), ("step", 8), ("step", 9),
 ]
 PATTERN = "iccic" * 5 + "ic" + "iiiii"
 FIRST, LAST = "c", "i"
@@ -173,6 +174,12 @@ def tile_layernormlstmcell_pa_kernel(
             for half in (0, 1):
                 vec[(nm, half)] = vec_sb[nm][:, 2 * half * NT : 2 * (half + 1) * NT]
 
+        def load_quarter(nm, t):
+            cols = slice(t * NT, (t + 1) * NT)
+            nc.sync.dma_start(out=vec_sb[nm][:, cols], in_=vec_src[nm][cols].partition_broadcast(P))
+            for half in (0, 1):
+                vec[(nm, half)] = vec_sb[nm][:, 2 * half * NT : 2 * (half + 1) * NT]
+
         def spread(nm, half):
             j = vec_names.index(nm)
             ps = psum.tile([P, 2 * NT], BF16, name="tp", tag="tp", bufs=TP_BUFS)
@@ -216,6 +223,11 @@ def tile_layernormlstmcell_pa_kernel(
         keyed = [(-9.0, ("scale", 0)), (-8.0, ("step", 0)), (-7.0, ("act", "x")), (-6.0, ("scale", 1)), (1.5, ("act", "h"))]
         keyed += [(SC2_KEY, ("scale", 2)), (SC2_KEY + 0.01, ("scale", 3)), (VEC_KEYS[0], ("vec", "gain_" + FIRST)), (VEC_KEYS[1], ("vec", "shift_" + FIRST))]
         keyed += [(i - (BYTE_LEAD if steps[i][0] == "Wi" else 0.0), ("step", i)) for i in range(1, n_steps)]
+        keyed += [(12.6, ("rows", 0))]
+        for g in ("i", "c"):
+            for t in range(4):
+                closes = max(i for i in range(n_steps) if steps[i][0][1] == g and steps[i][1] == t)
+                keyed += [(closes + 1 + BIAS_LEAD, ("quarter", ("bias_" + g, t)))]
         plan = [e[1] for e in sorted(keyed)]
         if HEAD_ORDER:
             plan = list(HEAD_ORDER) + [e for e in plan if e not in HEAD_ORDER]
@@ -234,6 +246,8 @@ def tile_layernormlstmcell_pa_kernel(
                     load_act(what)
                 elif kind == "rows":
                     load_rows()
+                elif kind == "quarter":
+                    load_quarter(what[0], what[1])
                 else:
                     load_vec(what)
                 plan_at["i"] += 1

@@ -18,6 +18,8 @@ K = 2048
 H = 2048
 NT = 512
 KS = 1024
+NS = 256
+PASSES = 4
 EPS = 1e-5
 FLOPS = 2 * 128 * 4096 * 4096
 
@@ -73,7 +75,7 @@ def tile_layernormlstmcell_pa_kernel(
     units_upto = {}
     for j in range(len(wi_steps)):
         width = NT if j < FINE_STEPS else KS
-        units += [(wi_steps[j], r, c0, width) for c0 in range(0, KS, width) for r in range(4)]
+        units += [(wi_steps[j], r, c0, width) for c0 in range(0, K, width) for r in range(2)]
         units_upto[wi_steps[j]] = len(units)
 
     with ExitStack() as ctx:
@@ -206,17 +208,16 @@ def tile_layernormlstmcell_pa_kernel(
             return n < RAW_BUFS or raw_hist[n - RAW_BUFS] in turned
 
         def fetch(i):
-            m, t, kh = steps[i]
-            rows = slice(t * NT, (t + 1) * NT)
-            cols = slice(kh * KS, (kh + 1) * KS)
+            m, t, hf = steps[i]
+            rows = slice(t * NT + hf * NS, t * NT + (hf + 1) * NS)
             if m == "Wi":
-                wi_bytes = byte_pool.tile([P, 4, KS], U8, name="wi_bytes")
-                nc.sync.dma_start(out=wi_bytes[:], in_=Wi_w_bytes[rows, cols].rearrange("(r p) k -> p r k", p=P))
+                wi_bytes = byte_pool.tile([P, 2, K], U8, name="wi_bytes")
+                nc.sync.dma_start(out=wi_bytes[:], in_=Wi_w_bytes[rows, :].rearrange("(r p) k -> p r k", p=P))
                 byt[i] = wi_bytes
                 byte_hist.append(i)
             else:
-                raw = raw_pool.tile([P, 4, KS], BF16, name="raw")
-                nc.sync.dma_start(out=raw[:], in_=weights[m][rows, cols].rearrange("(r p) k -> p r k", p=P))
+                raw = raw_pool.tile([P, 2, K], BF16, name="raw")
+                nc.sync.dma_start(out=raw[:], in_=weights[m][rows, :].rearrange("(r p) k -> p r k", p=P))
                 src[i] = raw
                 raw_hist.append(i)
 
@@ -263,36 +264,16 @@ def tile_layernormlstmcell_pa_kernel(
             if i not in src:
                 if j >= WIDE_BUFS and wi_steps[j - WIDE_BUFS] not in turned:
                     return 0
-                wide = wide_pool.tile([P, 4, KS], BF16, name="wide")
+                wide = wide_pool.tile([P, 2, K], BF16, name="wide")
                 src[i] = wide
-            kh = steps[i][2]
             nc.vector.tensor_tensor(
                 out=src[i][:, r, c0 : c0 + width],
                 in0=byt[i][:, r, c0 : c0 + width].bitcast(FP8),
-                in1=scale_bc[:, kh * KS + c0 : kh * KS + c0 + width],
+                in1=scale_bc[:, c0 : c0 + width],
                 op=ALU.mult,
             )
             widened["unit"] = u + 1
             return width // NT
-
-        def sort_one(first):
-            for i in (first, first + 1):
-                if i >= n_steps or i not in src or i in turned:
-                    continue
-                if steps[i][0] == "Wi" and widened["unit"] < units_upto[i]:
-                    continue
-                for r in range(4):
-                    if (i, r) not in sorted_blocks:
-                        if i not in srt:
-                            s_t = sort_pool.tile([P, 4, 2, 2, P], F32, name="sorted")
-                            srt[i] = s_t
-                        nc.vector.tensor_copy(
-                            out=srt[i][:, r, :, :, :],
-                            in_=src[i][:].bitcast(F32)[:, r, :].rearrange("p (g j u) -> p g u j", g=2, u=2),
-                        )
-                        sorted_blocks.add((i, r))
-                        return True
-            return False
 
         def turn_bank(word_aps, grp_words, b):
             tp = psum.tile([P, 2, 2 * P], F32, name="tp", tag="tp", bufs=TP_BUFS)
@@ -301,24 +282,16 @@ def tile_layernormlstmcell_pa_kernel(
                     nc.tensor.transpose(out=tp[:, u, l * P : (l + 1) * P], in_=word_aps[l][u], identity=ident[:])
             nc.scalar.copy(out=grp_words[:, 2 * P * b : 2 * P * (b + 1), :], in_=tp[:].rearrange("p u c -> p c u"))
 
-        def words_of(i, r, gl, u):
-            if (i, r) in sorted_blocks:
-                return srt[i][:, r, gl, u, :]
-            return src[i][:].bitcast(F32)[:, r, 256 * gl + u : 256 * (gl + 1) : 2]
-
-        def turn(i, halfway=None):
-            g_t = grp_pool.tile([P, 2, 4 * NT], BF16, name="grp", align_bytes=64)
+        def turn(i, after_bank=None):
+            g_t = grp_pool.tile([P, PASSES, 4 * NS], BF16, name="grp", align_bytes=64)
             grp[i] = g_t
-            banks = [(gl, b) for gl in (0, 1) for b in (0, 1)]
-            if steps[i][0] == "Wi" and wi_steps.index(i) >= FINE_STEPS:
-                banks = [(gl, b) for b in (0, 1) for gl in (0, 1)]
-            for n_bank in range(4):
-                gl, b = banks[n_bank]
-                grp_words = g_t[:, gl, :].bitcast(F32).rearrange("p (c u) -> p c u", u=2)
-                aps = [[words_of(i, 2 * b + l, gl, u) for u in (0, 1)] for l in (0, 1)]
-                turn_bank(aps, grp_words, b)
-                if n_bank == 1 and halfway:
-                    halfway()
+            words = src[i][:].bitcast(F32)
+            for kp in range(PASSES):
+                grp_words = g_t[:, kp, :].bitcast(F32).rearrange("p (c u) -> p c u", u=2)
+                aps = [[words[:, l, 256 * kp + u : 256 * (kp + 1) : 2] for u in (0, 1)] for l in (0, 1)]
+                turn_bank(aps, grp_words, 0)
+                if after_bank:
+                    after_bank(kp)
             turned.add(i)
 
         def turn_act(nm):
@@ -341,32 +314,35 @@ def tile_layernormlstmcell_pa_kernel(
             if i + 1 < n_steps:
                 nc.vector.quantize_mx(out=c_t[:].bitcast(FP8X4), scales=s_t[:], in_=grp[i][:].rearrange("p g c -> p (g c)"))
             else:
-                for gl in (0, 1):
-                    cols = slice(gl * NT, (gl + 1) * NT)
-                    nc.vector.quantize_mx(out=c_t[:, cols].bitcast(FP8X4), scales=s_t[:, cols], in_=grp[i][:, gl, :])
+                for half in (0, 1):
+                    cols = slice(half * NT, (half + 1) * NT)
+                    nc.vector.quantize_mx(
+                        out=c_t[:, cols].bitcast(FP8X4), scales=s_t[:, cols], in_=grp[i][:, 2 * half : 2 * half + 2, :].rearrange("p g c -> p (g c)")
+                    )
 
-        def multiply(i, gl, slot):
-            m, t, kh = steps[i]
+        def multiply(i, kp, slot):
+            m, t, hf = steps[i]
             g = m[1]
             a = "x" if m[0] == "W" else "h"
-            done = passes.get((g, t), 0)
-            if done == 0:
+            done = passes.get((g, t, hf), 0)
+            if done == 0 and hf == 0:
                 assert t == 0 or ("empty", g, t - 1) in flags
                 bank = FIRST if (SWAP_BANK and g == LAST and t == 3) else g
                 acc_t = psum.tile([P, NT], F32, name="acc_" + bank, tag="acc_" + bank, bufs=1)
                 acc[(g, t)] = acc_t
-            kp = 2 * kh + gl
+            if hf == 1:
+                assert passes[(g, t, 0)] == 8
             nc.tensor.matmul_mx(
-                out=acc[(g, t)][:],
+                out=acc[(g, t)][:, hf * NS : (hf + 1) * NS],
                 lhsT=act_codes[a][:, kp * P : (kp + 1) * P].bitcast(FP8X4),
                 lhsT_scale=act_scales[a][:, kp * P : (kp + 1) * P],
-                rhs=codes[i][:, gl * NT : (gl + 1) * NT].bitcast(FP8X4),
-                rhs_scale=scales[i][:, gl * NT : (gl + 1) * NT],
+                rhs=codes[i][:, kp * NS : (kp + 1) * NS].bitcast(FP8X4),
+                rhs_scale=scales[i][:, kp * NS : (kp + 1) * NS],
                 start=(done == 0),
                 stop=(done == 7),
             )
-            passes[(g, t)] = done + 1
-            if done == 7 and not (g == LAST and t == 3):
+            passes[(g, t, hf)] = done + 1
+            if done == 7 and hf == 1 and not (g == LAST and t == 3):
                 urgent.append([3 * (slot + 1), (), lambda: empty(g, t)])
                 if t == 3:
                     sjobs.append([("empty", g, 3), lambda: mean_on_scalar(g)])
@@ -532,7 +508,7 @@ def tile_layernormlstmcell_pa_kernel(
                 vfill(3 * s)
             if s + 2 < n_steps:
                 ready(s + 2)
-                turn(s + 2, lambda: multiply(s, 0, s))
+                turn(s + 2, lambda kp: multiply(s, kp, s))
             if s + 1 < n_steps:
                 quantize(s + 1)
             if s == 0:
@@ -543,8 +519,8 @@ def tile_layernormlstmcell_pa_kernel(
             if s + 1 == n_steps:
                 spread("gain_" + LAST, 0)
             if s + 2 >= n_steps:
-                multiply(s, 0, s)
-            multiply(s, 1, s)
+                for kp in range(PASSES):
+                    multiply(s, kp, s)
             issue_loads(s + 2)
         spread("gain_" + LAST, 1)
         spread("shift_" + LAST, 0)

@@ -484,6 +484,11 @@ def tile_layernormlstmcell_pa_kernel(
                 while widened["unit"] < units_upto[i]:
                     assert widen_one()
 
+        def pair_of_passes(s, kp):
+            if kp % 2 == 1:
+                multiply(s, kp - 1, s)
+                multiply(s, kp, s)
+
         issue_loads(0)
         turn_scales()
         for q in range(4):
@@ -508,7 +513,7 @@ def tile_layernormlstmcell_pa_kernel(
                 vfill(3 * s)
             if s + 2 < n_steps:
                 ready(s + 2)
-                turn(s + 2, lambda kp: multiply(s, kp, s))
+                turn(s + 2, lambda kp: pair_of_passes(s, kp))
             if s + 1 < n_steps:
                 quantize(s + 1)
             if s == 0:

@@ -29,11 +29,16 @@ SC2_KEY = -1.6
 RAW_BUFS = 6
 BYTE_BUFS = 4
 WIDE_BUFS = 3
-SORT_BUFS = 3
+SORT_BUFS = 1
 GRP_BUFS = 2
 CODE_BUFS = 3
 TP_BUFS = 6
-SORT_CAP = 0
+SORT_EVERY = 2
+VPOS = 3
+LN_TO = 28
+SORT_PHASE = 0
+SORT_LEAD = 4
+SORT_TO = 0
 SORT_FROM = 0
 VEC_KEYS = (23.1, 25.1)
 BIAS_LEAD = 2.5
@@ -125,8 +130,8 @@ def tile_layernormlstmcell_pa_kernel(
         small = {}
         for g in ("i", "c"):
             pre[g] = const.tile([P, H], F32, name="pre_" + g)
-            sums[g] = const.tile([P, 4], F32, name="sums_" + g)
-            ssq[g] = const.tile([P, 4], F32, name="ssq_" + g)
+            sums[g] = const.tile([P, 8], F32, name="sums_" + g)
+            ssq[g] = const.tile([P, 8], F32, name="ssq_" + g)
             for nm in ("negc", "s012", "m012", "q012", "e0", "mean", "d", "e", "ve", "rstd"):
                 small[nm + g] = const.tile([P, 1], F32, name=nm + "_" + g)
 
@@ -146,7 +151,9 @@ def tile_layernormlstmcell_pa_kernel(
         vjobs = []
         urgent = []
         sjobs = []
-        flags = set()
+        slow = []
+        flags = {}
+        now = {"slot": 0}
 
         def load_scale(c):
             if c == 0:
@@ -282,6 +289,14 @@ def tile_layernormlstmcell_pa_kernel(
                     nc.tensor.transpose(out=tp[:, u, l * P : (l + 1) * P], in_=word_aps[l][u], identity=ident[:])
             nc.scalar.copy(out=grp_words[:, 2 * P * b : 2 * P * (b + 1), :], in_=tp[:].rearrange("p u c -> p c u"))
 
+        def sort_words(i):
+            s_t = sort_pool.tile([P, K // 2], F32, name="sorted")
+            srt[i] = s_t
+            nc.vector.tensor_copy(
+                out=s_t[:].rearrange("p (g u c) -> p g u c", u=2, c=P),
+                in_=src[i][:, 1, :].bitcast(F32).rearrange("p (g c u) -> p g u c", u=2, c=P),
+            )
+
         def turn(i, after_bank=None):
             g_t = grp_pool.tile([P, PASSES, 4 * NS], BF16, name="grp", align_bytes=64)
             grp[i] = g_t
@@ -289,6 +304,8 @@ def tile_layernormlstmcell_pa_kernel(
             for kp in range(PASSES):
                 grp_words = g_t[:, kp, :].bitcast(F32).rearrange("p (c u) -> p c u", u=2)
                 aps = [[words[:, l, 256 * kp + u : 256 * (kp + 1) : 2] for u in (0, 1)] for l in (0, 1)]
+                if i in srt:
+                    aps[1] = [srt[i][:, 256 * kp + P * u : 256 * kp + P * (u + 1)] for u in (0, 1)]
                 turn_bank(aps, grp_words, 0)
                 if after_bank:
                     after_bank(kp)
@@ -314,11 +331,9 @@ def tile_layernormlstmcell_pa_kernel(
             if i + 1 < n_steps:
                 nc.vector.quantize_mx(out=c_t[:].bitcast(FP8X4), scales=s_t[:], in_=grp[i][:].rearrange("p g c -> p (g c)"))
             else:
-                for half in (0, 1):
-                    cols = slice(half * NT, (half + 1) * NT)
-                    nc.vector.quantize_mx(
-                        out=c_t[:, cols].bitcast(FP8X4), scales=s_t[:, cols], in_=grp[i][:, 2 * half : 2 * half + 2, :].rearrange("p g c -> p (g c)")
-                    )
+                for kp in range(PASSES):
+                    cols = slice(kp * NS, (kp + 1) * NS)
+                    nc.vector.quantize_mx(out=c_t[:, cols].bitcast(FP8X4), scales=s_t[:, cols], in_=grp[i][:, kp, :])
 
         def multiply(i, kp, slot):
             m, t, hf = steps[i]
@@ -344,45 +359,40 @@ def tile_layernormlstmcell_pa_kernel(
             passes[(g, t, hf)] = done + 1
             if done == 7 and hf == 1 and not (g == LAST and t == 3):
                 urgent.append([3 * (slot + 1), (), lambda: empty(g, t)])
-                if t == 3:
-                    sjobs.append([("empty", g, 3), lambda: mean_on_scalar(g)])
                 sjobs.append([("empty", g, t), lambda: squares(g, t)])
-                if t == 2:
-                    sjobs.append([("squares", g, 2), lambda: partial_sums(g)])
+                if t == 2 and g == FIRST:
+                    sjobs.append([("squares", g, 2), lambda: partial_sums(g, 3)])
                 if t == 3:
                     sjobs.append([("squares", g, 3), lambda: rstd_on_scalar(g)])
                     gate_jobs(g, slot + 1)
 
-        def empty(g, t):
-            cols = slice(t * NT, (t + 1) * NT)
+        def empty(g, t, a=0, b=NT, col=None):
+            col = t if col is None else col
+            cols = slice(t * NT + a, t * NT + b)
             nc.vector.scalar_tensor_tensor(
-                out=pre[g][:, cols], in0=acc[(g, t)][:], scalar=1.0, in1=vcols("bias_" + g, t),
-                op0=ALU.mult, op1=ALU.add, accum_out=sums[g][:, t : t + 1],
+                out=pre[g][:, cols], in0=acc[(g, t)][:, a:b], scalar=1.0, in1=vcols("bias_" + g, t)[:, a:b],
+                op0=ALU.mult, op1=ALU.add, accum_out=sums[g][:, col : col + 1],
             )
-            flags.add(("empty", g, t))
+            flags.setdefault(("empty", g, t), now["slot"])
 
-        def squares(g, t):
-            cols = slice(t * NT, (t + 1) * NT)
+        def squares(g, t, a=0, b=NT, col=None):
+            col = t if col is None else col
+            cols = slice(t * NT + a, t * NT + b)
             junk = work.tile([P, NT], BF16, name="junk", bufs=2)
             if t == 0:
                 nc.scalar.activation(out=small["negc" + g][:], in_=sums[g][:, 0:1], func=ACT.Copy, scale=-1.0 / NT)
             nc.scalar.activation(
-                out=junk[:], in_=pre[g][:, cols], func=ACT.Square, bias=small["negc" + g][:], scale=1.0,
-                accum_out=ssq[g][:, t : t + 1],
+                out=junk[:, 0 : b - a], in_=pre[g][:, cols], func=ACT.Square, bias=small["negc" + g][:], scale=1.0,
+                accum_out=ssq[g][:, col : col + 1],
             )
-            flags.add(("squares", g, t))
+            flags.setdefault(("squares", g, t), now["slot"])
 
-        def partial_sums(g):
+        def partial_sums(g, n):
             j_s = work.tile([P, 4], F32, name="junk_s", bufs=2)
-            nc.scalar.activation(out=j_s[:, 0:3], in_=sums[g][:, 0:3], func=ACT.Copy, scale=1.0 / H, accum_out=small["m012" + g][:])
+            nc.scalar.activation(out=j_s[:, 0:n], in_=sums[g][:, 0:n], func=ACT.Copy, scale=1.0 / H, accum_out=small["m012" + g][:])
             j_q = work.tile([P, 4], F32, name="junk_q", bufs=2)
-            nc.scalar.activation(out=j_q[:, 0:3], in_=ssq[g][:, 0:3], func=ACT.Copy, scale=1.0 / H, bias=EPS / 3.0, accum_out=small["e0" + g][:])
-            flags.add(("partial", g))
-
-        def mean_on_scalar(g):
-            assert ("partial", g) in flags
-            nc.scalar.activation(out=small["mean" + g][:], in_=sums[g][:, 3:4], func=ACT.Identity, scale=1.0 / H, bias=small["m012" + g][:])
-            flags.add(("mean", g))
+            nc.scalar.activation(out=j_q[:, 0:n], in_=ssq[g][:, 0:n], func=ACT.Copy, scale=1.0 / H, bias=EPS / n, accum_out=small["e0" + g][:])
+            flags.setdefault(("partial", g), now["slot"])
 
         def rstd_on_scalar(g):
             assert ("squares", g, 3) in flags
@@ -391,16 +401,16 @@ def tile_layernormlstmcell_pa_kernel(
             nc.scalar.activation(out=small["e" + g][:], in_=ssq[g][:, 3:4], func=ACT.Identity, scale=1.0 / H, bias=small["e0" + g][:])
             nc.scalar.activation(out=small["ve" + g][:], in_=small["s012" + g][:], func=ACT.Identity, scale=-1.0, bias=small["e" + g][:])
             nc.gpsimd.tensor_tensor(out=small["rstd" + g][:], in0=small["ve" + g][:], in1=neg_half[:], op=ALU.pow)
-            flags.add(("rstd", g))
+            flags.setdefault(("rstd", g), now["slot"])
 
         cen = {}
-        aff = {}
         th = {}
 
-        def mean_of(g):
+        def mean_of(g, col):
             assert ("partial", g) in flags
+            flags.setdefault(("mean", g), now["slot"])
             nc.vector.scalar_tensor_tensor(
-                out=small["mean" + g][:], in0=sums[g][:, 3:4], scalar=1.0 / H, in1=small["m012" + g][:], op0=ALU.mult, op1=ALU.add
+                out=small["mean" + g][:], in0=sums[g][:, col : col + 1], scalar=1.0 / H, in1=small["m012" + g][:], op0=ALU.mult, op1=ALU.add
             )
 
         def shift_of(g):
@@ -414,55 +424,54 @@ def tile_layernormlstmcell_pa_kernel(
         def rstd_of(g):
             assert ("squares", g, 3) in flags
             nc.vector.scalar_tensor_tensor(
-                out=small["ve" + g][:], in0=ssq[g][:, 3:4], scalar=1.0 / H, in1=small["e" + g][:], op0=ALU.mult, op1=ALU.subtract
+                out=small["ve" + g][:], in0=ssq[g][:, 4:5], scalar=1.0 / H, in1=small["e" + g][:], op0=ALU.mult, op1=ALU.subtract
             )
             nc.gpsimd.tensor_tensor(out=small["rstd" + g][:], in0=small["ve" + g][:], in1=neg_half[:], op=ALU.pow)
 
         def centre(g, t):
             cols = slice(t * NT, (t + 1) * NT)
-            c_t = work.tile([P, NT], F32, name="cen", bufs=4)
+            c_t = work.tile([P, NT], F32, name="cen", bufs=6)
             cen[(g, t)] = c_t
             nc.vector.scalar_tensor_tensor(
                 out=c_t[:], in0=pre[g][:, cols], scalar=small["mean" + g][:], in1=vcols("gain_" + g, t), op0=ALU.subtract, op1=ALU.mult
             )
-            flags.add(("centre", g, t))
+            flags.setdefault(("centre", g, t), now["slot"])
 
-        def affine(g, t):
-            cols = slice(t * NT, (t + 1) * NT)
-            a_t = work.tile([P, NT], F32, name="aff", bufs=3)
-            aff[(g, t)] = a_t
+        def affine(g, t, a=0, b=NT):
             nc.vector.scalar_tensor_tensor(
-                out=a_t[:], in0=cen[(g, t)][:], scalar=small["rstd" + g][:], in1=vcols("shift_" + g, t), op0=ALU.mult, op1=ALU.add
+                out=cen[(g, t)][:, a:b], in0=cen[(g, t)][:, a:b], scalar=small["rstd" + g][:], in1=vcols("shift_" + g, t)[:, a:b], op0=ALU.mult, op1=ALU.add
             )
-            flags.add(("affine", g, t))
+            flags.setdefault(("affine", g, t), now["slot"])
 
-        def squash(g, t):
+        def squash(g, t, a=0, b=NT):
             func = ACT.Sigmoid if g == "i" else ACT.Tanh
             if g == FIRST:
-                nc.scalar.activation(out=pre[g][:, t * NT : (t + 1) * NT], in_=aff[(g, t)][:], func=func)
+                nc.scalar.activation(out=pre[g][:, t * NT + a : t * NT + b], in_=cen[(g, t)][:, a:b], func=func)
             else:
-                t_t = work.tile([P, NT], F32, name="th", bufs=4)
-                th[t] = t_t
-                nc.scalar.activation(out=t_t[:], in_=aff[(g, t)][:], func=func)
+                if t not in th:
+                    t_t = work.tile([P, NT], F32, name="th", bufs=4)
+                    th[t] = t_t
+                nc.scalar.activation(out=th[t][:, a:b], in_=cen[(g, t)][:, a:b], func=func)
 
-        def product(t):
-            cols = slice(t * NT, (t + 1) * NT)
-            o_t = work.tile([P, NT], F32, name="o", bufs=4)
+        def product(t, a=0, b=NT):
+            cols = slice(t * NT + a, t * NT + b)
+            o_t = work.tile([P, NT], F32, name="o", bufs=5)
             eng = nc.gpsimd if t in GP_PRODUCTS else nc.vector
-            eng.tensor_tensor(out=o_t[:], in0=pre[FIRST][:, cols], in1=th[t][:], op=ALU.mult)
-            nc.sync.dma_start(out=out[:, cols], in_=o_t[:])
+            eng.tensor_tensor(out=o_t[:, 0 : b - a], in0=pre[FIRST][:, cols], in1=th[t][:, a:b], op=ALU.mult)
+            nc.sync.dma_start(out=out[:, cols], in_=o_t[:, 0 : b - a])
 
         def gate_jobs(g, slot):
+            vjobs.append([3 * slot, ("empty", g, 3), lambda: mean_of(g, 3)])
             for t in range(4):
-                vjobs.append([3 * slot + 1 + t, ("mean", g), lambda t=t: centre(g, t)])
+                vjobs.append([3 * slot + t // 2, ("mean", g), lambda t=t: centre(g, t)])
             for t in range(4):
                 vjobs.append([3 * slot + 5 + t, ("rstd", g), lambda t=t: affine(g, t)])
-                sjobs.append([("affine", g, t), lambda t=t: squash(g, t)])
+                slow.append([("affine", g, t), lambda t=t: squash(g, t)])
 
         widen_left = {"n": 0}
 
         def vfill(pos):
-            able = [j for j in urgent + vjobs if j[0] <= pos and (not j[1] or j[1] in flags)]
+            able = [j for j in urgent + (vjobs if pos < 3 * (LN_TO + 1) else []) if j[0] <= pos and (not j[1] or j[1] in flags)]
             if able:
                 if able[0] in urgent:
                     urgent.remove(able[0])
@@ -472,11 +481,16 @@ def tile_layernormlstmcell_pa_kernel(
             elif widen_left["n"] > 0:
                 widen_left["n"] -= widen_one()
 
-        def sfill(n):
+        def sfill(n, lag=1):
             for k in range(n):
                 able = [j for j in sjobs if j[0] in flags]
                 if able:
                     sjobs.remove(able[0])
+                    able[0][1]()
+                    continue
+                able = [j for j in slow if j[0] in flags and flags[j[0]] + lag <= now["slot"] and not n_steps - 5 < now["slot"] < n_steps]
+                if able:
+                    slow.remove(able[0])
                     able[0][1]()
 
         def ready(i):
@@ -507,55 +521,71 @@ def tile_layernormlstmcell_pa_kernel(
         quantize(0)
         widen_one()
         issue_loads(1)
-        for s in range(n_steps):
+        for s in range(n_steps - 2):
+            now["slot"] = s
             widen_left["n"] = WIDEN_CAP
             while [j for j in urgent if j[0] <= 3 * s]:
                 vfill(3 * s)
-            if s + 2 < n_steps:
-                ready(s + 2)
-                turn(s + 2, lambda kp: pair_of_passes(s, kp))
-            if s + 1 < n_steps:
-                quantize(s + 1)
+            ready(s + 2)
+            turn(s + 2, lambda kp: pair_of_passes(s, kp))
+            quantize(s + 1)
             if s == 0:
                 quantize_act("h")
-            for k in range(3):
+            for k in range(VPOS):
                 vfill(3 * s + k)
                 sfill(1)
-            if s + 1 == n_steps:
-                spread("gain_" + LAST, 0)
-            if s + 2 >= n_steps:
-                for kp in range(PASSES):
-                    multiply(s, kp, s)
+            if SORT_FROM <= s < SORT_TO and s % SORT_EVERY == SORT_PHASE and s + SORT_LEAD < n_steps and s + SORT_LEAD in src and steps[s + SORT_LEAD][0] != "Wi":
+                sort_words(s + SORT_LEAD)
             issue_loads(s + 2)
-        spread("gain_" + LAST, 1)
-        spread("shift_" + LAST, 0)
-        spread("shift_" + LAST, 1)
 
-        for k in range(len(vjobs)):
-            vfill(3 * n_steps)
-        assert not vjobs and not urgent, len(vjobs)
+        now["slot"] = n_steps
         g = LAST
-        empty(g, 3)
-        mean_of(g)
-        squares(g, 3)
-        sfill(16)
-        assert not sjobs
-        centre(g, 0)
+        for kp in range(PASSES):
+            multiply(n_steps - 2, kp, n_steps - 2)
+        sfill(len(sjobs), 99)
+        while urgent:
+            urgent.pop(0)[2]()
+        quantize(n_steps - 1)
+        empty(g, 3, 0, NS, 3)
+        squares(g, 3, 0, NS, 3)
+        partial_sums(g, 4)
+        for kp in range(PASSES):
+            multiply(n_steps - 1, kp, n_steps - 1)
+        for nm in ("gain_" + g, "shift_" + g):
+            spread(nm, 0)
+            spread(nm, 1)
+        late = [j[2] for j in vjobs]
+        for job in late[:1]:
+            job()
+        empty(g, 3, NS, NT, 4)
+        for job in late[1:2]:
+            job()
+        mean_of(g, 4)
+        squares(g, 3, NS, NT, 4)
+        sfill(4, 0)
         shift_of(g)
-        centre(g, 1)
+        centre(g, 0)
         shift_sq(g)
+        for job in late[2:3]:
+            job()
         rstd_of(g)
-        centre(g, 2)
+        centre(g, 1)
         affine(g, 0)
         squash(g, 0)
+        for job in late[3:]:
+            job()
+        sfill(16, 0)
+        product(0)
+        centre(g, 2)
         affine(g, 1)
         squash(g, 1)
-        product(0)
+        product(1)
         centre(g, 3)
         affine(g, 2)
         squash(g, 2)
-        product(1)
-        affine(g, 3)
-        squash(g, 3)
+        for half in (0, 1):
+            affine(g, 3, half * NS, (half + 1) * NS)
+            squash(g, 3, half * NS, (half + 1) * NS)
         product(2)
-        product(3)
+        product(3, 0, NS)
+        product(3, NS, NT)

@@ -40,7 +40,7 @@ SORT_PHASE = 0
 SORT_LEAD = 4
 SORT_TO = 0
 SORT_FROM = 0
-VEC_KEYS = (23.1, 25.1)
+VEC_KEYS = (31.6, 31.8)
 BIAS_LEAD = 2.5
 HEAD_ORDER = [
     ("scale", 0), ("step", 0), ("act", "x"), ("scale", 1), ("step", 1), ("act", "h"), ("step", 2), ("scale", 2), ("scale", 3), ("step", 5),
@@ -340,15 +340,18 @@ def tile_layernormlstmcell_pa_kernel(
             g = m[1]
             a = "x" if m[0] == "W" else "h"
             done = passes.get((g, t, hf), 0)
-            if done == 0 and hf == 0:
+            last_tile = g == LAST and t == 3
+            if done == 0 and (hf == 0 or last_tile):
                 assert t == 0 or ("empty", g, t - 1) in flags
-                bank = FIRST if (SWAP_BANK and g == LAST and t == 3) else g
+                bank = FIRST if last_tile and hf == 0 else g
                 acc_t = psum.tile([P, NT], F32, name="acc_" + bank, tag="acc_" + bank, bufs=1)
-                acc[(g, t)] = acc_t
+                acc[(g, t, hf)] = acc_t
+                if not last_tile:
+                    acc[(g, t, 1)] = acc_t
             if hf == 1:
                 assert passes[(g, t, 0)] == 8
             nc.tensor.matmul_mx(
-                out=acc[(g, t)][:, hf * NS : (hf + 1) * NS],
+                out=acc[(g, t, hf)][:, hf * NS : (hf + 1) * NS],
                 lhsT=act_codes[a][:, kp * P : (kp + 1) * P].bitcast(FP8X4),
                 lhsT_scale=act_scales[a][:, kp * P : (kp + 1) * P],
                 rhs=codes[i][:, kp * NS : (kp + 1) * NS].bitcast(FP8X4),
@@ -370,7 +373,7 @@ def tile_layernormlstmcell_pa_kernel(
             col = t if col is None else col
             cols = slice(t * NT + a, t * NT + b)
             nc.vector.scalar_tensor_tensor(
-                out=pre[g][:, cols], in0=acc[(g, t)][:, a:b], scalar=1.0, in1=vcols("bias_" + g, t)[:, a:b],
+                out=pre[g][:, cols], in0=acc[(g, t, a // NS)][:, a:b], scalar=1.0, in1=vcols("bias_" + g, t)[:, a:b],
                 op0=ALU.mult, op1=ALU.add, accum_out=sums[g][:, col : col + 1],
             )
             flags.setdefault(("empty", g, t), now["slot"])

from contextlib import ExitStack

import concourse.masks as masks
import concourse.mybir as mybir

F32 = mybir.dt.float32
BF16 = mybir.dt.bfloat16
U32 = mybir.dt.uint32
U8 = mybir.dt.uint8
FP8 = mybir.dt.float8_e4m3fn
FP8X4 = mybir.dt.float8_e4m3fn_x4
ALU = mybir.AluOpType
ACT = mybir.ActivationFunctionType
AX = mybir.AxisListType

P = 128
K = 2048
H = 2048
NT = 512
KS = 1024
NS = 256
PASSES = 4
EPS = 1e-5
FLOPS = 2 * 128 * 4096 * 4096

AHEAD = 6
BYTE_LEAD = 5.5
SC2_KEY = -1.6
RAW_BUFS = 6
BYTE_BUFS = 4
WIDE_BUFS = 3
SORT_BUFS = 1
GRP_BUFS = 2
CODE_BUFS = 3
TP_BUFS = 6
SORT_EVERY = 2
VPOS = 3
LN_TO = 28
SORT_PHASE = 0
SORT_LEAD = 4
SORT_TO = 0
SORT_FROM = 0
VEC_KEYS = (31.6, 31.8)
BIAS_LEAD = 2.5
HEAD_ORDER = [
    ("scale", 0), ("step", 0), ("act", "x"), ("scale", 1), ("step", 1), ("act", "h"), ("step", 2), ("scale", 2), ("scale", 3), ("step", 5),
    ("step", 3), ("step", 4), ("step", 6), ("step", 10), ("step", 7), ("step", 8), ("step", 9),
]
PATTERN = "iccic" * 5 + "ic" + "iiiii"
FIRST, LAST = "c", "i"
WIDEN_CAP = 2
FINE_STEPS = 1
UW = 512
PER = 4 * (KS // UW)
BIAS_DMA = True
GP_PRODUCTS = (0, 1)
SWAP_BANK = True


def step_order():
    i_seq = [(m, t, kh) for t in range(4) for kh in (0, 1) for m in ("Wi", "Ui")]
    c_seq = [(m, t, kh) for t in range(4) for kh in (0, 1) for m in ("Wc", "Uc")]
    order = []
    for ch in PATTERN:
        seq = i_seq if ch == "i" else c_seq
        order.append(seq[0])
        seq.remove(seq[0])
    return order


def tile_layernormlstmcell_pa_kernel(
    tc, x, h, Wi_w_bytes, Wi_w_scale, Wi_b, Ui_w, lni_g, lni_b, Wc_w, Wc_b, Uc_w, lnc_g, lnc_b, out
):
    nc = tc.nc
    steps = step_order()
    n_steps = len(steps)
    weights = {"Ui": Ui_w, "Wc": Wc_w, "Uc": Uc_w}
    wi_steps = [i for i in range(n_steps) if steps[i][0] == "Wi"]
    units = []
    units_upto = {}
    for j in range(len(wi_steps)):
        width = NT if j < FINE_STEPS else KS
        units += [(wi_steps[j], r, c0, width) for c0 in range(0, K, width) for r in range(2)]
        units_upto[wi_steps[j]] = len(units)

    with ExitStack() as ctx:
        const = ctx.enter_context(tc.tile_pool(name="const", bufs=1))
        raw_pool = ctx.enter_context(tc.tile_pool(name="raw", bufs=RAW_BUFS))
        byte_pool = ctx.enter_context(tc.tile_pool(name="bytes", bufs=BYTE_BUFS))
        wide_pool = ctx.enter_context(tc.tile_pool(name="wide", bufs=WIDE_BUFS))
        sort_pool = ctx.enter_context(tc.tile_pool(name="sorted", bufs=SORT_BUFS))
        grp_pool = ctx.enter_context(tc.tile_pool(name="grp", bufs=GRP_BUFS))
        code_pool = ctx.enter_context(tc.tile_pool(name="code", bufs=CODE_BUFS))
        work = ctx.enter_context(tc.tile_pool(name="work", bufs=3))
        psum = ctx.enter_context(tc.psum_pool(name="psum", bufs=1))
        ctx.enter_context(tc.manual_schedule())

        scale_rows = const.tile([P, P], F32, name="scale_rows")
        nc.gpsimd.memset(scale_rows[:], 0.0)
        ident = const.tile([P, P], F32, name="ident")
        masks.make_identity(nc, ident[:])
        neg_half = const.tile([P, 1], F32, name="neg_half")
        nc.gpsimd.memset(neg_half[:], -0.5)
        warm = const.tile([P, 1], F32, name="warm")
        nc.scalar.activation(out=warm[:], in_=neg_half[:], func=ACT.Sigmoid)

        scale_bc = const.tile([P, K], F32, name="scale_bc")
        scale_cols = const.tile([P, 16], F32, name="scale_cols")
        vec_src = {"bias_i": Wi_b, "bias_c": Wc_b, "gain_i": lni_g, "gain_c": lnc_g, "shift_i": lni_b, "shift_c": lnc_b}
        vec_names = ("bias_i", "bias_c", "gain_" + FIRST, "shift_" + FIRST, "gain_" + LAST, "shift_" + LAST)
        ident_bf = const.tile([P, P], BF16, name="ident_bf")
        masks.make_identity(nc, ident_bf[:])
        vrows = const.tile([P, H], BF16, name="vrows")
        nc.vector.memset(vrows[:], 0.0)
        vec = {}
        vec_sb = {}
        for nm in vec_names[:4]:
            vec_sb[nm] = const.tile([P, H], BF16, name=nm)
        act_src = {"x": x, "h": h}
        act_sb = {}
        act_codes = {}
        act_scales = {}
        for nm in ("x", "h"):
            act_sb[nm] = const.tile([P, K], BF16, name=nm + "_sb")
            act_codes[nm] = const.tile([P, NT], U32, name=nm + "_codes", align_bytes=64)
            act_scales[nm] = const.tile([P, NT], U8, name=nm + "_scales", align_bytes=64)
        pre = {}
        sums = {}
        ssq = {}
        small = {}
        for g in ("i", "c"):
            pre[g] = const.tile([P, H], F32, name="pre_" + g)
            sums[g] = const.tile([P, 8], F32, name="sums_" + g)
            ssq[g] = const.tile([P, 8], F32, name="ssq_" + g)
            for nm in ("negc", "s012", "m012", "q012", "e0", "mean", "d", "e", "ve", "rstd"):
                small[nm + g] = const.tile([P, 1], F32, name=nm + "_" + g)

        src = {}
        byt = {}
        srt = {}
        sorted_blocks = set()
        grp = {}
        codes = {}
        scales = {}
        acc = {}
        passes = {}
        turned = set()
        raw_hist = []
        byte_hist = []
        widened = {"unit": 0}
        vjobs = []
        urgent = []
        sjobs = []
        slow = []
        flags = {}
        now = {"slot": 0}

        def load_scale(c):
            if c == 0:
                nc.sync.dma_start(out=scale_rows[0:16, :], in_=Wi_w_scale.rearrange("o (c j) -> (o c) j", j=P))

        def turn_scales():
            tp = psum.tile([P, 2, 2 * P], F32, name="tp", tag="tp", bufs=TP_BUFS)
            nc.tensor.transpose(out=tp[:, 0, 0:P], in_=scale_rows[:], identity=ident[:])
            nc.scalar.copy(out=scale_cols[:], in_=tp[:, 0, 0:16])

        def spread_scales(q):
            tp = psum.tile([P, 2, 2 * P], F32, name="tp", tag="tp", bufs=TP_BUFS)
            for l in range(4):
                c = 4 * q + l
                nc.tensor.transpose(out=tp[:, l // 2, (l % 2) * P : (l % 2 + 1) * P], in_=scale_cols[:, c : c + 1].to_broadcast([P, P]), identity=ident[:])
            nc.scalar.copy(out=scale_bc[:, q * NT : (q + 1) * NT], in_=tp[:].rearrange("p a b -> p (a b)"))

        def load_act(nm):
            nc.sync.dma_start(out=act_sb[nm][:], in_=act_src[nm])

        def load_rows():
            for j in (4, 5) if BIAS_DMA else (0, 1, 4, 5):
                nc.sync.dma_start(out=vrows[j : j + 1, :], in_=vec_src[vec_names[j]].unsqueeze(0))

        def load_vec(nm):
            nc.sync.dma_start(out=vec_sb[nm][:], in_=vec_src[nm].partition_broadcast(P))
            for half in (0, 1):
                vec[(nm, half)] = vec_sb[nm][:, 2 * half * NT : 2 * (half + 1) * NT]

        def load_quarter(nm, t):
            cols = slice(t * NT, (t + 1) * NT)
            nc.sync.dma_start(out=vec_sb[nm][:, cols], in_=vec_src[nm][cols].partition_broadcast(P))
            for half in (0, 1):
                vec[(nm, half)] = vec_sb[nm][:, 2 * half * NT : 2 * (half + 1) * NT]

        def spread(nm, half):
            j = vec_names.index(nm)
            ps = psum.tile([P, 2 * NT], BF16, name="tp", tag="tp", bufs=TP_BUFS)
            for q in (0, 1):
                c0 = (2 * half + q) * NT
                nc.tensor.matmul(
                    out=ps[:, q * NT : (q + 1) * NT], lhsT=ident_bf[:, j : j + 1].to_broadcast([P, P]), rhs=vrows[:, c0 : c0 + NT],
                    start=True, stop=True,
                )
            if nm in vec_sb:
                nc.scalar.copy(out=vec_sb[nm][:, 2 * half * NT : 2 * (half + 1) * NT], in_=ps[:])
                vec[(nm, half)] = vec_sb[nm][:, 2 * half * NT : 2 * (half + 1) * NT]
            else:
                vec[(nm, half)] = ps

        def vcols(nm, t):
            return vec[(nm, t // 2)][:, (t % 2) * NT : (t % 2 + 1) * NT]

        def can_fetch(i):
            if steps[i][0] == "Wi":
                n = len(byte_hist)
                return n < BYTE_BUFS or widened["unit"] >= units_upto[byte_hist[n - BYTE_BUFS]]
            n = len(raw_hist)
            return n < RAW_BUFS or raw_hist[n - RAW_BUFS] in turned

        def fetch(i):
            m, t, hf = steps[i]
            rows = slice(t * NT + hf * NS, t * NT + (hf + 1) * NS)
            if m == "Wi":
                wi_bytes = byte_pool.tile([P, 2, K], U8, name="wi_bytes")
                nc.sync.dma_start(out=wi_bytes[:], in_=Wi_w_bytes[rows, :].rearrange("(r p) k -> p r k", p=P))
                byt[i] = wi_bytes
                byte_hist.append(i)
            else:
                raw = raw_pool.tile([P, 2, K], BF16, name="raw")
                nc.sync.dma_start(out=raw[:], in_=weights[m][rows, :].rearrange("(r p) k -> p r k", p=P))
                src[i] = raw
                raw_hist.append(i)

        keyed = [(-9.0, ("scale", 0)), (-8.0, ("step", 0)), (-7.0, ("act", "x")), (-6.0, ("scale", 1)), (1.5, ("act", "h"))]
        keyed += [(SC2_KEY, ("scale", 2)), (SC2_KEY + 0.01, ("scale", 3)), (VEC_KEYS[0], ("vec", "gain_" + FIRST)), (VEC_KEYS[1], ("vec", "shift_" + FIRST))]
        keyed += [(i - (BYTE_LEAD if steps[i][0] == "Wi" else 0.0), ("step", i)) for i in range(1, n_steps)]
        keyed += [(12.6, ("rows", 0))]
        for g in ("i", "c"):
            for t in range(4):
                closes = max(i for i in range(n_steps) if steps[i][0][1] == g and steps[i][1] == t)
                keyed += [(closes + 1 + BIAS_LEAD, ("quarter", ("bias_" + g, t)))]
        plan = [e[1] for e in sorted(keyed)]
        if HEAD_ORDER:
            plan = list(HEAD_ORDER) + [e for e in plan if e not in HEAD_ORDER]
        plan_at = {"i": 0}

        def issue_loads(slot):
            while plan_at["i"] < len(plan):
                kind, what = plan[plan_at["i"]]
                if kind == "step":
                    if what > slot + AHEAD + (BYTE_LEAD if steps[what][0] == "Wi" else 0) or not can_fetch(what):
                        return
                    fetch(what)
                elif kind == "scale":
                    load_scale(what)
                elif kind == "act":
                    load_act(what)
                elif kind == "rows":
                    load_rows()
                elif kind == "quarter":
                    load_quarter(what[0], what[1])
                else:
                    load_vec(what)
                plan_at["i"] += 1

        def widen_one():
            u = widened["unit"]
            if u >= len(units):
                return 0
            i, r, c0, width = units[u]
            j = wi_steps.index(i)
            if i not in byt:
                return 0
            if i not in src:
                if j >= WIDE_BUFS and wi_steps[j - WIDE_BUFS] not in turned:
                    return 0
                wide = wide_pool.tile([P, 2, K], BF16, name="wide")
                src[i] = wide
            nc.vector.tensor_tensor(
                out=src[i][:, r, c0 : c0 + width],
                in0=byt[i][:, r, c0 : c0 + width].bitcast(FP8),
                in1=scale_bc[:, c0 : c0 + width],
                op=ALU.mult,
            )
            widened["unit"] = u + 1
            return width // NT

        def turn_bank(word_aps, grp_words, b):
            tp = psum.tile([P, 2, 2 * P], F32, name="tp", tag="tp", bufs=TP_BUFS)
            for l in (0, 1):
                for u in (0, 1):
                    nc.tensor.transpose(out=tp[:, u, l * P : (l + 1) * P], in_=word_aps[l][u], identity=ident[:])
            nc.scalar.copy(out=grp_words[:, 2 * P * b : 2 * P * (b + 1), :], in_=tp[:].rearrange("p u c -> p c u"))

        def sort_words(i):
            s_t = sort_pool.tile([P, K // 2], F32, name="sorted")
            srt[i] = s_t
            nc.vector.tensor_copy(
                out=s_t[:].rearrange("p (g u c) -> p g u c", u=2, c=P),
                in_=src[i][:, 1, :].bitcast(F32).rearrange("p (g c u) -> p g u c", u=2, c=P),
            )

        def turn(i, after_bank=None):
            g_t = grp_pool.tile([P, PASSES, 4 * NS], BF16, name="grp", align_bytes=64)
            grp[i] = g_t
            words = src[i][:].bitcast(F32)
            for kp in range(PASSES):
                grp_words = g_t[:, kp, :].bitcast(F32).rearrange("p (c u) -> p c u", u=2)
                aps = [[words[:, l, 256 * kp + u : 256 * (kp + 1) : 2] for u in (0, 1)] for l in (0, 1)]
                if i in srt:
                    aps[1] = [srt[i][:, 256 * kp + P * u : 256 * kp + P * (u + 1)] for u in (0, 1)]
                turn_bank(aps, grp_words, 0)
                if after_bank:
                    after_bank(kp)
            turned.add(i)

        def turn_act(nm):
            words = act_sb[nm][:].bitcast(F32)
            g_t = const.tile([P, 4 * NT], BF16, name="grp_" + nm, align_bytes=64)
            grp[nm] = g_t
            grp_words = g_t[:].bitcast(F32).rearrange("p (c u) -> p c u", u=2)
            for b in (0, 1):
                aps = [[words[:, 256 * (2 * b + l) + u : 256 * (2 * b + l + 1) : 2] for u in (0, 1)] for l in (0, 1)]
                turn_bank(aps, grp_words, b)

        def quantize_act(nm):
            nc.vector.quantize_mx(out=act_codes[nm][:].bitcast(FP8X4), scales=act_scales[nm][:], in_=grp[nm][:])

        def quantize(i):
            c_t = code_pool.tile([P, 2 * NT], U32, name="codes", align_bytes=64)
            s_t = code_pool.tile([P, 2 * NT], U8, name="scales", align_bytes=64)
            codes[i] = c_t
            scales[i] = s_t
            if i + 1 < n_steps:
                nc.vector.quantize_mx(out=c_t[:].bitcast(FP8X4), scales=s_t[:], in_=grp[i][:].rearrange("p g c -> p (g c)"))
            else:
                for kp in range(PASSES):
                    cols = slice(kp * NS, (kp + 1) * NS)
                    nc.vector.quantize_mx(out=c_t[:, cols].bitcast(FP8X4), scales=s_t[:, cols], in_=grp[i][:, kp, :])

        def multiply(i, kp, slot):
            m, t, hf = steps[i]
            g = m[1]
            a = "x" if m[0] == "W" else "h"
            done = passes.get((g, t, hf), 0)
            last_tile = g == LAST and t == 3
            if done == 0 and (hf == 0 or last_tile):
                assert t == 0 or ("empty", g, t - 1) in flags
                bank = FIRST if last_tile and hf == 0 else g
                acc_t = psum.tile([P, NT], F32, name="acc_" + bank, tag="acc_" + bank, bufs=1)
                acc[(g, t, hf)] = acc_t
                if not last_tile:
                    acc[(g, t, 1)] = acc_t
            if hf == 1:
                assert passes[(g, t, 0)] == 8
            nc.tensor.matmul_mx(
                out=acc[(g, t, hf)][:, hf * NS : (hf + 1) * NS],
                lhsT=act_codes[a][:, kp * P : (kp + 1) * P].bitcast(FP8X4),
                lhsT_scale=act_scales[a][:, kp * P : (kp + 1) * P],
                rhs=codes[i][:, kp * NS : (kp + 1) * NS].bitcast(FP8X4),
                rhs_scale=scales[i][:, kp * NS : (kp + 1) * NS],
                start=(done == 0),
                stop=(done == 7),
            )
            passes[(g, t, hf)] = done + 1
            if done == 7 and hf == 1 and not (g == LAST and t == 3):
                urgent.append([3 * (slot + 1), (), lambda: empty(g, t)])
                sjobs.append([("empty", g, t), lambda: squares(g, t)])
                if t == 2 and g == FIRST:
                    sjobs.append([("squares", g, 2), lambda: partial_sums(g, 3)])
                if t == 3:
                    sjobs.append([("squares", g, 3), lambda: rstd_on_scalar(g)])
                    gate_jobs(g, slot + 1)

        def empty(g, t, a=0, b=NT, col=None):
            col = t if col is None else col
            cols = slice(t * NT + a, t * NT + b)
            nc.vector.scalar_tensor_tensor(
                out=pre[g][:, cols], in0=acc[(g, t, a // NS)][:, a:b], scalar=1.0, in1=vcols("bias_" + g, t)[:, a:b],
                op0=ALU.mult, op1=ALU.add, accum_out=sums[g][:, col : col + 1],
            )
            flags.setdefault(("empty", g, t), now["slot"])

        def squares(g, t, a=0, b=NT, col=None):
            col = t if col is None else col
            cols = slice(t * NT + a, t * NT + b)
            junk = work.tile([P, NT], BF16, name="junk", bufs=2)
            if t == 0:
                nc.scalar.activation(out=small["negc" + g][:], in_=sums[g][:, 0:1], func=ACT.Copy, scale=-1.0 / NT)
            nc.scalar.activation(
                out=junk[:, 0 : b - a], in_=pre[g][:, cols], func=ACT.Square, bias=small["negc" + g][:], scale=1.0,
                accum_out=ssq[g][:, col : col + 1],
            )
            flags.setdefault(("squares", g, t), now["slot"])

        def partial_sums(g, n):
            j_s = work.tile([P, 4], F32, name="junk_s", bufs=2)
            nc.scalar.activation(out=j_s[:, 0:n], in_=sums[g][:, 0:n], func=ACT.Copy, scale=1.0 / H, accum_out=small["m012" + g][:])
            j_q = work.tile([P, 4], F32, name="junk_q", bufs=2)
            nc.scalar.activation(out=j_q[:, 0:n], in_=ssq[g][:, 0:n], func=ACT.Copy, scale=1.0 / H, bias=EPS / n, accum_out=small["e0" + g][:])
            flags.setdefault(("partial", g), now["slot"])

        def rstd_on_scalar(g):
            assert ("squares", g, 3) in flags
            nc.scalar.activation(out=small["d" + g][:], in_=small["mean" + g][:], func=ACT.Identity, scale=1.0, bias=small["negc" + g][:])
            nc.scalar.activation(out=small["s012" + g][:], in_=small["d" + g][:], func=ACT.Square)
            nc.scalar.activation(out=small["e" + g][:], in_=ssq[g][:, 3:4], func=ACT.Identity, scale=1.0 / H, bias=small["e0" + g][:])
            nc.scalar.activation(out=small["ve" + g][:], in_=small["s012" + g][:], func=ACT.Identity, scale=-1.0, bias=small["e" + g][:])
            nc.gpsimd.tensor_tensor(out=small["rstd" + g][:], in0=small["ve" + g][:], in1=neg_half[:], op=ALU.pow)
            flags.setdefault(("rstd", g), now["slot"])

        cen = {}
        th = {}

        def mean_of(g, col):
            assert ("partial", g) in flags
            flags.setdefault(("mean", g), now["slot"])
            nc.vector.scalar_tensor_tensor(
                out=small["mean" + g][:], in0=sums[g][:, col : col + 1], scalar=1.0 / H, in1=small["m012" + g][:], op0=ALU.mult, op1=ALU.add
            )

        def shift_of(g):
            nc.vector.tensor_tensor(out=small["d" + g][:], in0=small["mean" + g][:], in1=small["negc" + g][:], op=ALU.add)

        def shift_sq(g):
            nc.vector.scalar_tensor_tensor(
                out=small["e" + g][:], in0=small["d" + g][:], scalar=small["d" + g][:], in1=small["e0" + g][:], op0=ALU.mult, op1=ALU.subtract
            )

        def rstd_of(g):
            assert ("squares", g, 3) in flags
            nc.vector.scalar_tensor_tensor(
                out=small["ve" + g][:], in0=ssq[g][:, 4:5], scalar=1.0 / H, in1=small["e" + g][:], op0=ALU.mult, op1=ALU.subtract
            )
            nc.gpsimd.tensor_tensor(out=small["rstd" + g][:], in0=small["ve" + g][:], in1=neg_half[:], op=ALU.pow)

        def centre(g, t):
            cols = slice(t * NT, (t + 1) * NT)
            c_t = work.tile([P, NT], F32, name="cen", bufs=6)
            cen[(g, t)] = c_t
            nc.vector.scalar_tensor_tensor(
                out=c_t[:], in0=pre[g][:, cols], scalar=small["mean" + g][:], in1=vcols("gain_" + g, t), op0=ALU.subtract, op1=ALU.mult
            )
            flags.setdefault(("centre", g, t), now["slot"])

        def affine(g, t, a=0, b=NT):
            nc.vector.scalar_tensor_tensor(
                out=cen[(g, t)][:, a:b], in0=cen[(g, t)][:, a:b], scalar=small["rstd" + g][:], in1=vcols("shift_" + g, t)[:, a:b], op0=ALU.mult, op1=ALU.add
            )
            flags.setdefault(("affine", g, t), now["slot"])

        def squash(g, t, a=0, b=NT):
            func = ACT.Sigmoid if g == "i" else ACT.Tanh
            if g == FIRST:
                nc.scalar.activation(out=pre[g][:, t * NT + a : t * NT + b], in_=cen[(g, t)][:, a:b], func=func)
            else:
                if t not in th:
                    t_t = work.tile([P, NT], F32, name="th", bufs=4)
                    th[t] = t_t
                nc.scalar.activation(out=th[t][:, a:b], in_=cen[(g, t)][:, a:b], func=func)

        def product(t, a=0, b=NT):
            cols = slice(t * NT + a, t * NT + b)
            o_t = work.tile([P, NT], F32, name="o", bufs=5)
            eng = nc.gpsimd if t in GP_PRODUCTS else nc.vector
            eng.tensor_tensor(out=o_t[:, 0 : b - a], in0=pre[FIRST][:, cols], in1=th[t][:, a:b], op=ALU.mult)
            nc.sync.dma_start(out=out[:, cols], in_=o_t[:, 0 : b - a])

        def gate_jobs(g, slot):
            vjobs.append([3 * slot, ("empty", g, 3), lambda: mean_of(g, 3)])
            for t in range(4):
                vjobs.append([3 * slot + t // 2, ("mean", g), lambda t=t: centre(g, t)])
            for t in range(4):
                vjobs.append([3 * slot + 5 + t, ("rstd", g), lambda t=t: affine(g, t)])
                slow.append([("affine", g, t), lambda t=t: squash(g, t)])

        widen_left = {"n": 0}

        def vfill(pos):
            able = [j for j in urgent + (vjobs if pos < 3 * (LN_TO + 1) else []) if j[0] <= pos and (not j[1] or j[1] in flags)]
            if able:
                if able[0] in urgent:
                    urgent.remove(able[0])
                else:
                    vjobs.remove(able[0])
                able[0][2]()
            elif widen_left["n"] > 0:
                widen_left["n"] -= widen_one()

        def sfill(n, lag=1):
            for k in range(n):
                able = [j for j in sjobs if j[0] in flags]
                if able:
                    sjobs.remove(able[0])
                    able[0][1]()
                    continue
                able = [j for j in slow if j[0] in flags and flags[j[0]] + lag <= now["slot"] and not n_steps - 5 < now["slot"] < n_steps]
                if able:
                    slow.remove(able[0])
                    able[0][1]()

        def ready(i):
            if steps[i][0] == "Wi":
                while widened["unit"] < units_upto[i]:
                    assert widen_one()

        def pair_of_passes(s, kp):
            if kp % 2 == 1:
                multiply(s, kp - 1, s)
                multiply(s, kp, s)

        issue_loads(0)
        turn_scales()
        for q in range(4):
            spread_scales(q)
        for k in range(8):
            widen_one()
        turn_act("x")
        quantize_act("x")
        turn(0)
        for nm in () if BIAS_DMA else ("bias_i", "bias_c"):
            spread(nm, 0)
            spread(nm, 1)
        ready(1)
        turn(1)
        turn_act("h")
        quantize(0)
        widen_one()
        issue_loads(1)
        for s in range(n_steps - 2):
            now["slot"] = s
            widen_left["n"] = WIDEN_CAP
            while [j for j in urgent if j[0] <= 3 * s]:
                vfill(3 * s)
            ready(s + 2)
            turn(s + 2, lambda kp: pair_of_passes(s, kp))
            quantize(s + 1)
            if s == 0:
                quantize_act("h")
            for k in range(VPOS):
                vfill(3 * s + k)
                sfill(1)
            if SORT_FROM <= s < SORT_TO and s % SORT_EVERY == SORT_PHASE and s + SORT_LEAD < n_steps and s + SORT_LEAD in src and steps[s + SORT_LEAD][0] != "Wi":
                sort_words(s + SORT_LEAD)
            issue_loads(s + 2)

        now["slot"] = n_steps
        g = LAST
        for kp in range(PASSES):
            multiply(n_steps - 2, kp, n_steps - 2)
        sfill(len(sjobs), 99)
        while urgent:
            urgent.pop(0)[2]()
        quantize(n_steps - 1)
        empty(g, 3, 0, NS, 3)
        squares(g, 3, 0, NS, 3)
        partial_sums(g, 4)
        for kp in range(PASSES):
            multiply(n_steps - 1, kp, n_steps - 1)
        for nm in ("gain_" + g, "shift_" + g):
            spread(nm, 0)
            spread(nm, 1)
        late = [j[2] for j in vjobs]
        for job in late[:1]:
            job()
        empty(g, 3, NS, NT, 4)
        for job in late[1:2]:
            job()
        mean_of(g, 4)
        squares(g, 3, NS, NT, 4)
        sfill(4, 0)
        shift_of(g)
        centre(g, 0)
        shift_sq(g)
        for job in late[2:3]:
            job()
        rstd_of(g)
        centre(g, 1)
        affine(g, 0)
        squash(g, 0)
        for job in late[3:]:
            job()
        sfill(16, 0)
        product(0)
        centre(g, 2)
        affine(g, 1)
        squash(g, 1)
        product(1)
        centre(g, 3)
        affine(g, 2)
        squash(g, 2)
        for half in (0, 1):
            affine(g, 3, half * NS, (half + 1) * NS)
            squash(g, 3, half * NS, (half + 1) * NS)
        product(2)
        product(3, 0, NS)
        product(3, NS, NT)
